import numpy as np
import ml_dtypes


def mxq(x, axis, fmt="e4m3"):
    dtype, down = {"e4m3": (ml_dtypes.float8_e4m3fn, 7), "e5m2": (ml_dtypes.float8_e5m2, 14)}[fmt]
    v = np.moveaxis(np.asarray(x, np.float32).astype(ml_dtypes.bfloat16).astype(np.float64), axis, -1)
    blocks = v.reshape(v.shape[:-1] + (-1, 32))
    amax = np.abs(blocks).max(-1, keepdims=True)
    byte = np.maximum(np.where(amax > 0, np.frexp(amax)[1] - 1 + 127, 0) - down, 1)
    scale = np.exp2(byte - 127.0)
    codes = (blocks / scale).astype(np.float32).astype(dtype).astype(np.float64)
    return np.moveaxis((codes * scale).reshape(v.shape), -1, axis)


WIDE = False


def mx_kscale(k):
    if not WIDE:
        return np.ones(k)
    levels = np.array([10, -10, 5, -5, 0])
    a = np.random.permutation(np.resize(levels, k // 512 * 4)).reshape(k // 512, 4)
    idx = np.arange(k)
    return np.exp2(a[idx // 512, idx % 128 // 32])


BF16 = ml_dtypes.bfloat16


def bf(x):
    return np.asarray(x, np.float32).astype(BF16)


def f64(x):
    return np.asarray(x).astype(np.float64)


B, S, D, F = 2, 512, 1024, 1024
LN_EPS = 1e-5


def layer_norm(x, gamma, beta):
    mu = x.mean(-1, keepdims=True)
    var = np.square(x - mu).mean(-1, keepdims=True)
    return (x - mu) / np.sqrt(var + LN_EPS) * gamma + beta


def setup_inputs():
    t = mx_kscale(F)
    return {"x_norm1": bf(np.random.standard_normal((B, S, D))),
            "W1": bf(np.random.standard_normal((F, D)) / np.sqrt(D) * t[:, None]),
            "b1": bf(0.2 * np.random.standard_normal(F) * t),
            "W2": bf(np.random.standard_normal((D, F)) / np.sqrt(F) / t[None, :]),
            "b2": bf(0.2 * np.random.standard_normal(D)),
            "ln_gamma": bf(1.0 + 0.1 * np.random.standard_normal(D)),
            "ln_beta": bf(0.1 * np.random.standard_normal(D))}


def reference(x_norm1, W1, b1, W2, b2, ln_gamma, ln_beta):
    x = f64(x_norm1)
    h = np.maximum((mxq(x, 2, "e4m3") @ mxq(f64(W1), 1, "e4m3").T) + f64(b1), 0.0)
    ffn = (mxq(h, 2, "e4m3") @ mxq(f64(W2), 1, "e4m3").T) + f64(b2)
    return layer_norm(ffn + x, f64(ln_gamma), f64(ln_beta))

@@ -1,0 +1,274 @@
+from contextlib import ExitStack
+
+import concourse.mybir as mybir
+from concourse.masks import make_identity
+
+F32 = mybir.dt.float32
+BF16 = mybir.dt.bfloat16
+I32 = mybir.dt.int32
+U32 = mybir.dt.uint32
+U8 = mybir.dt.uint8
+FP8X4 = mybir.dt.float8_e4m3fn_x4
+FUNC = mybir.ActivationFunctionType
+ALU = mybir.AluOpType
+
+P = 128
+PACK = 4
+K_PASS = P * PACK
+BANK = 512
+
+TOKENS = 1024
+WIDTH = 1024
+PASSES = WIDTH // K_PASS
+ROW_TILES = 8
+CHUNK_TILES = 4
+CHUNK = CHUNK_TILES * P
+HALVES = TOKENS // CHUNK
+LN_EPS = 1e-5
+
+FLOPS = 2 * 2 * TOKENS * WIDTH * WIDTH
+
+
+def tile_transformerblock_pb_kernel(tc, x_norm1, W1, b1, W2, b2, ln_gamma, ln_beta, out):
+    nc = tc.nc
+    x_view = x_norm1.flatten_outer_dims().rearrange("(p i) d -> p i d", i=ROW_TILES)
+    out_view = out.flatten_outer_dims().rearrange("(p i) d -> p i d", i=ROW_TILES)
+
+    with ExitStack() as ctx:
+        keep = ctx.enter_context(tc.tile_pool(name="keep", bufs=1))
+        stage = ctx.enter_context(tc.tile_pool(name="stage", bufs=3))
+        hidden = ctx.enter_context(tc.tile_pool(name="hidden", bufs=2))
+        norm = ctx.enter_context(tc.tile_pool(name="norm", bufs=3))
+        small = ctx.enter_context(tc.tile_pool(name="small", bufs=4))
+        psum = ctx.enter_context(tc.psum_pool(name="psum", bufs=8))
+
+        ctx.enter_context(tc.manual_schedule())
+
+        vec_rows = keep.tile([P, 3 * WIDTH], BF16)
+        nc.vector.memset(vec_rows[:].bitcast(I32), 0)
+        for v, vec in enumerate((b2, ln_gamma, ln_beta)):
+            nc.sync.dma_start(
+                out=vec_rows[0:1, v * WIDTH : (v + 1) * WIDTH], in_=vec.rearrange("(o d) -> o d", o=1)
+            )
+
+        x_sb = keep.tile([P, ROW_TILES, WIDTH], BF16)
+        w1_sb = keep.tile([P, ROW_TILES, WIDTH], BF16)
+        w2_sb = keep.tile([P, ROW_TILES, WIDTH], BF16)
+        w1_view = W1.rearrange("(a p e) k -> p a (e k)", p=P, e=2)
+        w2_view = W2.rearrange("(j p) f -> p j f", p=P)
+
+        def chunk_tiles(c):
+            return slice(c * CHUNK_TILES, (c + 1) * CHUNK_TILES)
+
+        def load_x(c):
+            nc.sync.dma_start(out=x_sb[:, chunk_tiles(c), :], in_=x_view[:, chunk_tiles(c), :])
+
+        def load_w1(c):
+            nc.sync.dma_start(
+                out=w1_sb[:, chunk_tiles(c), :].rearrange("p (a e) k -> p a (e k)", e=2),
+                in_=w1_view[:, 2 * c : 2 * c + 2, :],
+            )
+
+        def load_w2(c):
+            nc.sync.dma_start(out=w2_sb[:, chunk_tiles(c), :], in_=w2_view[:, chunk_tiles(c), :])
+
+        load_x(0)
+        load_w1(0)
+        load_w1(1)
+        load_w2(0)
+        load_w2(1)
+        load_x(1)
+
+        b1_pairs = keep.tile([P, ROW_TILES], BF16)
+        with nc.allow_non_contiguous_dma(reason="b1 is 2 KiB, loaded once as 4-byte pairs"):
+            nc.scalar.dma_start(
+                out=b1_pairs[:].rearrange("p (a e) -> p a e", e=2),
+                in_=b1.rearrange("(a p e) -> p a e", p=P, e=2),
+            )
+        b1_col = keep.tile([P, ROW_TILES], F32)
+
+        ident = keep.tile([P, P], F32)
+        make_identity(nc, ident[:])
+        ones = keep.tile([P, P], BF16)
+        nc.vector.memset(ones[:], 1.0)
+        eps = keep.tile([P, 1], F32)
+        nc.vector.memset(eps[:], LN_EPS)
+        table_first = keep.tile([P, 1], F32)
+        nc.scalar.activation(out=table_first[:], in_=eps[:], func=FUNC.Sqrt)
+
+        vec_all = keep.tile([P, 3 * WIDTH], F32)
+        b2_all = vec_all[:, 0:WIDTH]
+        gamma_all = vec_all[:, WIDTH : 2 * WIDTH]
+        beta_all = vec_all[:, 2 * WIDTH : 3 * WIDTH]
+
+        def copy_out_of_psum(piece):
+            return nc.scalar.copy if piece % 2 == 0 else nc.vector.tensor_copy
+
+        def spread_vector(v):
+            for n in range(WIDTH // BANK):
+                cols = slice(v * WIDTH + n * BANK, v * WIDTH + (n + 1) * BANK)
+                spread = psum.tile([P, BANK], F32, tag="bank")
+                nc.tensor.matmul(spread[:], lhsT=ones[:], rhs=vec_rows[:, cols], start=True, stop=True)
+                copy_out_of_psum(n)(out=vec_all[:, cols], in_=spread[:])
+
+        x_codes = keep.tile([P, PASSES, TOKENS], U32, align_bytes=64)
+        x_scales = keep.tile([P, PASSES, TOKENS], U8, align_bytes=64)
+        w1_codes = keep.tile([P, PASSES, WIDTH], U32, align_bytes=64)
+        w1_scales = keep.tile([P, PASSES, WIDTH], U8, align_bytes=64)
+        w2_codes = keep.tile([P, PASSES, WIDTH], U32, align_bytes=64)
+        w2_scales = keep.tile([P, PASSES, WIDTH], U8, align_bytes=64)
+        h_codes = keep.tile([P, PASSES, TOKENS], U32, align_bytes=64)
+        h_scales = keep.tile([P, PASSES, TOKENS], U8, align_bytes=64)
+
+        def chunk_cols(c):
+            return slice(c * CHUNK, (c + 1) * CHUNK)
+
+        def pack_chunk(rows_sb, codes, scales, c):
+            grouped = stage.tile([P, PASSES * CHUNK * PACK], BF16, align_bytes=64)
+            grouped_words = grouped[:].bitcast(F32).rearrange("p (g r u) -> p g r u", g=PASSES, u=2)
+            for r in range(CHUNK_TILES):
+                words = rows_sb[:, c * CHUNK_TILES + r, :].bitcast(F32)
+                flipped = psum.tile([P, BANK], F32, tag="bank")
+                for gu in range(PASSES * 2):
+                    cols = slice(gu * P, (gu + 1) * P)
+                    nc.tensor.transpose(flipped[:, cols], words[:, cols], ident[:])
+                copy_out_of_psum(r)(
+                    out=grouped_words[:, :, r * P : (r + 1) * P, :],
+                    in_=flipped[:].rearrange("p (g u r) -> p g r u", g=PASSES, u=2),
+                )
+            for g in range(PASSES):
+                nc.vector.quantize_mx(
+                    out=codes[:, g, chunk_cols(c)].bitcast(FP8X4),
+                    scales=scales[:, g, chunk_cols(c)],
+                    in_=grouped[:, g * CHUNK * PACK : (g + 1) * CHUNK * PACK],
+                )
+
+        def hidden_tile(s, h_rows, j):
+            units = slice(j * P, (j + 1) * P)
+            acc = psum.tile([P, BANK], F32, tag="bank")
+            for g in range(PASSES):
+                nc.tensor.matmul_mx(
+                    out=acc[:],
+                    lhsT=w1_codes[:, g, units].bitcast(FP8X4),
+                    lhsT_scale=w1_scales[:, g, units],
+                    rhs=x_codes[:, g, chunk_cols(s)].bitcast(FP8X4),
+                    rhs_scale=x_scales[:, g, chunk_cols(s)],
+                    start=(g == 0),
+                    stop=(g == PASSES - 1),
+                )
+            nc.scalar.activation(
+                out=h_rows[:, j, :], in_=acc[:], func=FUNC.Relu, bias=b1_col[:, j : j + 1], scale=1.0
+            )
+
+        def regroup_hidden(h_rows, gf, regroup_copy):
+            h_grouped = hidden.tile([P, CHUNK * PACK], BF16, align_bytes=64)
+            regroup_copy(
+                out=h_grouped[:].rearrange("p (c i t) -> p c t i", i=4, t=PACK),
+                in_=h_rows[:, gf * PACK : (gf + 1) * PACK, :].rearrange("p t (c i) -> p c t i", i=4),
+            )
+            return h_grouped
+
+        def quantise_hidden(s, gf, h_grouped):
+            nc.vector.quantize_mx(
+                out=h_codes[:, gf, chunk_cols(s)].bitcast(FP8X4),
+                scales=h_scales[:, gf, chunk_cols(s)],
+                in_=h_grouped[:],
+            )
+
+        xb = keep.tile([P, ROW_TILES, WIDTH], F32)
+
+        def residual_plus_bias(i):
+            for n in range(WIDTH // BANK):
+                cols = slice(n * BANK, (n + 1) * BANK)
+                nc.gpsimd.tensor_tensor(out=xb[:, i, cols], in0=x_sb[:, i, cols], in1=b2_all[:, cols], op=ALU.add)
+
+        def start_tile(i):
+            tokens = slice(i * P, (i + 1) * P)
+            y = norm.tile([P, WIDTH], F32)
+            y_sum = small.tile([P, WIDTH // BANK], F32)
+            for n in range(WIDTH // BANK):
+                cols = slice(n * BANK, (n + 1) * BANK)
+                acc = psum.tile([P, BANK], F32, tag="bank")
+                for gf in range(PASSES):
+                    nc.tensor.matmul_mx(
+                        out=acc[:],
+                        lhsT=h_codes[:, gf, tokens].bitcast(FP8X4),
+                        lhsT_scale=h_scales[:, gf, tokens],
+                        rhs=w2_codes[:, gf, cols].bitcast(FP8X4),
+                        rhs_scale=w2_scales[:, gf, cols],
+                        start=(gf == 0),
+                        stop=(gf == PASSES - 1),
+                    )
+                nc.vector.scalar_tensor_tensor(
+                    out=y[:, cols], in0=acc[:], scalar=1.0, in1=xb[:, i, cols],
+                    op0=ALU.mult, op1=ALU.add, accum_out=y_sum[:, n : n + 1],
+                )
+            neg_mean = small.tile([P, 1], F32)
+            nc.vector.tensor_scalar(
+                out=neg_mean[:], in0=y_sum[:, 0:1], scalar1=y_sum[:, 1:2], scalar2=-1.0 / WIDTH,
+                op0=ALU.add, op1=ALU.mult,
+            )
+            squares = norm.tile([P, WIDTH], BF16)
+            sq_sum = small.tile([P, 1], F32)
+            nc.scalar.activation(
+                out=squares[:], in_=y[:], func=FUNC.Square, bias=neg_mean[:, 0:1], scale=1.0, accum_out=sq_sum[:]
+            )
+            std = small.tile([P, 1], F32)
+            nc.scalar.activation(out=std[:], in_=sq_sum[:], func=FUNC.Sqrt, bias=eps[:, 0:1], scale=1.0 / WIDTH)
+            z = norm.tile([P, WIDTH], F32)
+            nc.vector.scalar_tensor_tensor(
+                out=z[:], in0=y[:], scalar=neg_mean[:, 0:1], in1=gamma_all, op0=ALU.add, op1=ALU.mult
+            )
+            return z, std
+
+        def finish_tile(i, z, std):
+            rstd = small.tile([P, 1], F32)
+            nc.vector.reciprocal(out=rstd[:], in_=std[:])
+            nc.vector.scalar_tensor_tensor(
+                out=z[:], in0=z[:], scalar=rstd[:, 0:1], in1=beta_all, op0=ALU.mult, op1=ALU.add
+            )
+            nc.sync.dma_start(out=out_view[:, i, :], in_=z[:])
+
+        pack_chunk(x_sb, x_codes, x_scales, 0)
+        spread_vector(0)
+        for i in range(CHUNK_TILES):
+            residual_plus_bias(i)
+        pack_chunk(w1_sb, w1_codes, w1_scales, 0)
+        spread_vector(1)
+        pack_chunk(w1_sb, w1_codes, w1_scales, 1)
+        spread_vector(2)
+        nc.vector.tensor_copy(out=b1_col[:], in_=b1_pairs[:])
+        h_first = hidden.tile([P, ROW_TILES, CHUNK], BF16, tag="h_rows")
+        for gf in range(PASSES):
+            for t in range(PACK):
+                hidden_tile(0, h_first, gf * PACK + t)
+            quantise_hidden(0, gf, regroup_hidden(h_first, gf, nc.vector.tensor_copy))
+            pack_chunk(w2_sb, w2_codes, w2_scales, gf)
+        pack_chunk(x_sb, x_codes, x_scales, 1)
+        for i in range(CHUNK_TILES, ROW_TILES):
+            residual_plus_bias(i)
+
+        h_second = hidden.tile([P, ROW_TILES, CHUNK], BF16, tag="h_rows")
+        PAIRS = ROW_TILES // 2
+
+        def hidden_pair(k):
+            hidden_tile(1, h_second, 2 * k)
+            hidden_tile(1, h_second, 2 * k + 1)
+
+        hidden_pair(0)
+        started = None
+        regrouped = None
+        for i in range(ROW_TILES):
+            begun = start_tile(i)
+            if regrouped is not None:
+                quantise_hidden(1, *regrouped)
+                regrouped = None
+            if started is not None:
+                finish_tile(i - 1, *started)
+            started = begun
+            k = i + 1
+            if k < PAIRS:
+                hidden_pair(k)
+                if k % 2 == 1:
+                    regrouped = (k // 2, regroup_hidden(h_second, k // 2, nc.scalar.copy))
+        finish_tile(ROW_TILES - 1, *started)

@@ -42,7 +42,13 @@ def tile_transformerblock_pb_kernel(tc, x_norm1, W1, b1, W2, b2, ln_gamma, ln_be
         small = ctx.enter_context(tc.tile_pool(name="small", bufs=4))
         psum = ctx.enter_context(tc.psum_pool(name="psum", bufs=8))
 
-        ctx.enter_context(tc.manual_schedule())
+        b1_pairs = keep.tile([P, ROW_TILES], BF16)
+        with nc.allow_non_contiguous_dma(reason="b1 is 2 KiB, loaded once as 4-byte pairs"):
+            nc.scalar.dma_start(
+                out=b1_pairs[:].rearrange("p (a e) -> p a e", e=2),
+                in_=b1.rearrange("(a p e) -> p a e", p=P, e=2),
+            )
+        b1_col = keep.tile([P, ROW_TILES], F32)
 
         vec_rows = keep.tile([P, 3 * WIDTH], BF16)
         nc.vector.memset(vec_rows[:].bitcast(I32), 0)
@@ -79,14 +85,6 @@ def tile_transformerblock_pb_kernel(tc, x_norm1, W1, b1, W2, b2, ln_gamma, ln_be
         load_w2(1)
         load_x(1)
 
-        b1_pairs = keep.tile([P, ROW_TILES], BF16)
-        with nc.allow_non_contiguous_dma(reason="b1 is 2 KiB, loaded once as 4-byte pairs"):
-            nc.scalar.dma_start(
-                out=b1_pairs[:].rearrange("p (a e) -> p a e", e=2),
-                in_=b1.rearrange("(a p e) -> p a e", p=P, e=2),
-            )
-        b1_col = keep.tile([P, ROW_TILES], F32)
-
         ident = keep.tile([P, P], F32)
         make_identity(nc, ident[:])
         ones = keep.tile([P, P], BF16)
@@ -102,7 +100,7 @@ def tile_transformerblock_pb_kernel(tc, x_norm1, W1, b1, W2, b2, ln_gamma, ln_be
         beta_all = vec_all[:, 2 * WIDTH : 3 * WIDTH]
 
         def copy_out_of_psum(piece):
-            return nc.scalar.copy if piece % 2 == 0 else nc.vector.tensor_copy
+            return nc.any.tensor_copy
 
         def spread_vector(v):
             for n in range(WIDTH // BANK):
@@ -255,7 +253,6 @@ def tile_transformerblock_pb_kernel(tc, x_norm1, W1, b1, W2, b2, ln_gamma, ln_be
             hidden_tile(1, h_second, 2 * k)
             hidden_tile(1, h_second, 2 * k + 1)
 
-        hidden_pair(0)
         started = None
         regrouped = None
         for i in range(ROW_TILES):
@@ -266,6 +263,8 @@ def tile_transformerblock_pb_kernel(tc, x_norm1, W1, b1, W2, b2, ln_gamma, ln_be
             if started is not None:
                 finish_tile(i - 1, *started)
             started = begun
+            if i == 0:
+                hidden_pair(0)
             k = i + 1
             if k < PAIRS:
                 hidden_pair(k)

@@ -23,7 +23,6 @@ PASSES = WIDTH // K_PASS
 ROW_TILES = 8
 CHUNK_TILES = 4
 CHUNK = CHUNK_TILES * P
-HALVES = TOKENS // CHUNK
 LN_EPS = 1e-5
 
 FLOPS = 2 * 2 * TOKENS * WIDTH * WIDTH
@@ -38,24 +37,11 @@ def tile_transformerblock_pb_kernel(tc, x_norm1, W1, b1, W2, b2, ln_gamma, ln_be
         keep = ctx.enter_context(tc.tile_pool(name="keep", bufs=1))
         stage = ctx.enter_context(tc.tile_pool(name="stage", bufs=3))
         hidden = ctx.enter_context(tc.tile_pool(name="hidden", bufs=2))
-        norm = ctx.enter_context(tc.tile_pool(name="norm", bufs=3))
+        norm = ctx.enter_context(tc.tile_pool(name="norm", bufs=4))
         small = ctx.enter_context(tc.tile_pool(name="small", bufs=4))
-        psum = ctx.enter_context(tc.psum_pool(name="psum", bufs=8))
-
-        b1_pairs = keep.tile([P, ROW_TILES], BF16)
-        with nc.allow_non_contiguous_dma(reason="b1 is 2 KiB, loaded once as 4-byte pairs"):
-            nc.scalar.dma_start(
-                out=b1_pairs[:].rearrange("p (a e) -> p a e", e=2),
-                in_=b1.rearrange("(a p e) -> p a e", p=P, e=2),
-            )
-        b1_col = keep.tile([P, ROW_TILES], F32)
-
-        vec_rows = keep.tile([P, 3 * WIDTH], BF16)
-        nc.vector.memset(vec_rows[:].bitcast(I32), 0)
-        for v, vec in enumerate((b2, ln_gamma, ln_beta)):
-            nc.sync.dma_start(
-                out=vec_rows[0:1, v * WIDTH : (v + 1) * WIDTH], in_=vec.rearrange("(o d) -> o d", o=1)
-            )
+        psum = ctx.enter_context(tc.psum_pool(name="psum", bufs=6))
+        psum_keep = ctx.enter_context(tc.psum_pool(name="psum_keep", bufs=1))
+        ctx.enter_context(tc.manual_schedule())
 
         x_sb = keep.tile([P, ROW_TILES, WIDTH], BF16)
         w1_sb = keep.tile([P, ROW_TILES, WIDTH], BF16)
@@ -63,28 +49,40 @@ def tile_transformerblock_pb_kernel(tc, x_norm1, W1, b1, W2, b2, ln_gamma, ln_be
         w1_view = W1.rearrange("(a p e) k -> p a (e k)", p=P, e=2)
         w2_view = W2.rearrange("(j p) f -> p j f", p=P)
 
-        def chunk_tiles(c):
-            return slice(c * CHUNK_TILES, (c + 1) * CHUNK_TILES)
+        def load_x(first, last):
+            nc.sync.dma_start(out=x_sb[:, first:last, :], in_=x_view[:, first:last, :])
 
-        def load_x(c):
-            nc.sync.dma_start(out=x_sb[:, chunk_tiles(c), :], in_=x_view[:, chunk_tiles(c), :])
-
-        def load_w1(c):
+        def load_w1(first, last):
             nc.sync.dma_start(
-                out=w1_sb[:, chunk_tiles(c), :].rearrange("p (a e) k -> p a (e k)", e=2),
-                in_=w1_view[:, 2 * c : 2 * c + 2, :],
+                out=w1_sb[:, first:last, :].rearrange("p (a e) k -> p a (e k)", e=2),
+                in_=w1_view[:, first // 2 : last // 2, :],
             )
 
-        def load_w2(c):
-            nc.sync.dma_start(out=w2_sb[:, chunk_tiles(c), :], in_=w2_view[:, chunk_tiles(c), :])
+        def load_w2(first, last):
+            nc.sync.dma_start(out=w2_sb[:, first:last, :], in_=w2_view[:, first:last, :])
 
-        load_x(0)
-        load_w1(0)
-        load_w1(1)
-        load_w2(0)
-        load_w2(1)
-        load_x(1)
+        load_x(0, 2)
+        load_w1(0, 2)
+        load_w1(2, 4)
+        load_x(2, 4)
+        load_w1(4, 8)
+        load_x(4, 8)
+        load_w2(0, 4)
+        load_w2(4, 8)
 
+        vec_rows = keep.tile([P, 3 * WIDTH], BF16)
+        vec_bits = vec_rows[:].bitcast(I32)
+        nc.vector.memset(vec_bits, 0)
+        b1_pairs = keep.tile([P, ROW_TILES], BF16)
+        with nc.allow_non_contiguous_dma(reason="b1 is 2 KiB, loaded once as 4-byte pairs"):
+            nc.scalar.dma_start(
+                out=b1_pairs[:].rearrange("p (a e) -> p a e", e=2),
+                in_=b1.rearrange("(a p e) -> p a e", p=P, e=2),
+            )
+        for v, vec in enumerate((b2, ln_gamma, ln_beta)):
+            nc.scalar.dma_start(
+                out=vec_rows[0:1, v * WIDTH : (v + 1) * WIDTH], in_=vec.rearrange("(o d) -> o d", o=1)
+            )
         ident = keep.tile([P, P], F32)
         make_identity(nc, ident[:])
         ones = keep.tile([P, P], BF16)
@@ -92,22 +90,7 @@ def tile_transformerblock_pb_kernel(tc, x_norm1, W1, b1, W2, b2, ln_gamma, ln_be
         eps = keep.tile([P, 1], F32)
         nc.vector.memset(eps[:], LN_EPS)
         table_first = keep.tile([P, 1], F32)
-        nc.scalar.activation(out=table_first[:], in_=eps[:], func=FUNC.Sqrt)
-
-        vec_all = keep.tile([P, 3 * WIDTH], F32)
-        b2_all = vec_all[:, 0:WIDTH]
-        gamma_all = vec_all[:, WIDTH : 2 * WIDTH]
-        beta_all = vec_all[:, 2 * WIDTH : 3 * WIDTH]
-
-        def copy_out_of_psum(piece):
-            return nc.any.tensor_copy
-
-        def spread_vector(v):
-            for n in range(WIDTH // BANK):
-                cols = slice(v * WIDTH + n * BANK, v * WIDTH + (n + 1) * BANK)
-                spread = psum.tile([P, BANK], F32, tag="bank")
-                nc.tensor.matmul(spread[:], lhsT=ones[:], rhs=vec_rows[:, cols], start=True, stop=True)
-                copy_out_of_psum(n)(out=vec_all[:, cols], in_=spread[:])
+        nc.scalar.activation(out=table_first[:], in_=eps[:], func=FUNC.Abs_reciprocal_sqrt)
 
         x_codes = keep.tile([P, PASSES, TOKENS], U32, align_bytes=64)
         x_scales = keep.tile([P, PASSES, TOKENS], U8, align_bytes=64)
@@ -121,25 +104,70 @@ def tile_transformerblock_pb_kernel(tc, x_norm1, W1, b1, W2, b2, ln_gamma, ln_be
         def chunk_cols(c):
             return slice(c * CHUNK, (c + 1) * CHUNK)
 
-        def pack_chunk(rows_sb, codes, scales, c):
-            grouped = stage.tile([P, PASSES * CHUNK * PACK], BF16, align_bytes=64)
+        def flip(rows_sb, r):
+            words = rows_sb[:, r, :].bitcast(F32)
+            flipped = psum.tile([P, BANK], F32, tag="bank")
+            for gu in range(PASSES * 2):
+                cols = slice(gu * P, (gu + 1) * P)
+                nc.tensor.transpose(flipped[:, cols], words[:, cols], ident[:])
+            return flipped
+
+        def regroup(flipped, grouped, r, copy):
             grouped_words = grouped[:].bitcast(F32).rearrange("p (g r u) -> p g r u", g=PASSES, u=2)
-            for r in range(CHUNK_TILES):
-                words = rows_sb[:, c * CHUNK_TILES + r, :].bitcast(F32)
-                flipped = psum.tile([P, BANK], F32, tag="bank")
-                for gu in range(PASSES * 2):
-                    cols = slice(gu * P, (gu + 1) * P)
-                    nc.tensor.transpose(flipped[:, cols], words[:, cols], ident[:])
-                copy_out_of_psum(r)(
-                    out=grouped_words[:, :, r * P : (r + 1) * P, :],
-                    in_=flipped[:].rearrange("p (g u r) -> p g r u", g=PASSES, u=2),
-                )
+            copy(
+                out=grouped_words[:, :, r * P : (r + 1) * P, :],
+                in_=flipped[:].rearrange("p (g u r) -> p g r u", g=PASSES, u=2),
+            )
+
+        def quantise_rows(grouped, codes, scales, first, count):
             for g in range(PASSES):
+                cols = slice(first * P, (first + count) * P)
                 nc.vector.quantize_mx(
-                    out=codes[:, g, chunk_cols(c)].bitcast(FP8X4),
-                    scales=scales[:, g, chunk_cols(c)],
-                    in_=grouped[:, g * CHUNK * PACK : (g + 1) * CHUNK * PACK],
+                    out=codes[:, g, cols].bitcast(FP8X4),
+                    scales=scales[:, g, cols],
+                    in_=grouped[:, g * count * P * PACK : (g + 1) * count * P * PACK],
                 )
+
+        V = nc.vector.tensor_copy
+        S = nc.scalar.copy
+
+        def flip_rows(rows_sb, first, copies):
+            grouped = stage.tile([P, len(copies) * WIDTH], BF16, align_bytes=64, tag="grouped%d" % len(copies))
+            for r in range(len(copies)):
+                flipped = flip(rows_sb, first + r)
+                regroup(flipped, grouped, r, copies[r])
+            return grouped
+
+        def spread(v, store):
+            for n in range(WIDTH // BANK):
+                cols = slice(v * WIDTH + n * BANK, v * WIDTH + (n + 1) * BANK)
+                nc.tensor.matmul(
+                    store[:, n * BANK : (n + 1) * BANK], lhsT=ones[:], rhs=vec_rows[:, cols], start=True, stop=True
+                )
+
+        b1_col = keep.tile([P, ROW_TILES], F32)
+
+        def hidden_sum(i, gf, h_sum, k):
+            tokens = slice(i * P, (i + 1) * P)
+            acc = psum.tile([P, PACK, P], F32, tag="bank")
+            for t in range(PACK):
+                units = slice((gf * PACK + t) * P, (gf * PACK + t + 1) * P)
+                for g in range(PASSES):
+                    nc.tensor.matmul_mx(
+                        out=acc[:, t, :],
+                        lhsT=w1_codes[:, g, units].bitcast(FP8X4),
+                        lhsT_scale=w1_scales[:, g, units],
+                        rhs=x_codes[:, g, tokens].bitcast(FP8X4),
+                        rhs_scale=x_scales[:, g, tokens],
+                        start=(g == 0),
+                        stop=(g == PASSES - 1),
+                    )
+            nc.vector.tensor_tensor(
+                out=h_sum[:, k * BANK : (k + 1) * BANK].rearrange("p (n t) -> p n t", t=PACK),
+                in0=acc[:].rearrange("p t n -> p n t"),
+                in1=b1_col[:, gf * PACK : (gf + 1) * PACK].unsqueeze(1).to_broadcast([P, P, PACK]),
+                op=ALU.add,
+            )
 
         def hidden_tile(s, h_rows, j):
             units = slice(j * P, (j + 1) * P)
@@ -158,12 +186,21 @@ def tile_transformerblock_pb_kernel(tc, x_norm1, W1, b1, W2, b2, ln_gamma, ln_be
                 out=h_rows[:, j, :], in_=acc[:], func=FUNC.Relu, bias=b1_col[:, j : j + 1], scale=1.0
             )
 
-        def regroup_hidden(h_rows, gf, regroup_copy):
-            h_grouped = hidden.tile([P, CHUNK * PACK], BF16, align_bytes=64)
-            regroup_copy(
-                out=h_grouped[:].rearrange("p (c i t) -> p c t i", i=4, t=PACK),
-                in_=h_rows[:, gf * PACK : (gf + 1) * PACK, :].rearrange("p t (c i) -> p c t i", i=4),
-            )
+        def regroup_hidden(h_rows, gf, h_grouped, copies):
+            pieces = len(copies)
+            width = CHUNK // pieces
+            for n in range(pieces):
+                copies[n](
+                    out=h_grouped[:, n * width * PACK : (n + 1) * width * PACK].rearrange(
+                        "p (c i t) -> p c t i", i=4, t=PACK
+                    ),
+                    in_=h_rows[:, gf * PACK : (gf + 1) * PACK, n * width : (n + 1) * width].rearrange(
+                        "p t (c i) -> p c t i", i=4
+                    ),
+                )
+
+        def new_hidden():
+            h_grouped = hidden.tile([P, CHUNK * PACK], BF16, align_bytes=64, tag="h_grouped")
             return h_grouped
 
         def quantise_hidden(s, gf, h_grouped):
@@ -174,100 +211,214 @@ def tile_transformerblock_pb_kernel(tc, x_norm1, W1, b1, W2, b2, ln_gamma, ln_be
             )
 
         xb = keep.tile([P, ROW_TILES, WIDTH], F32)
+        b2_all = keep.tile([P, WIDTH], BF16)
+        gamma_all = psum_keep.tile([P, WIDTH], BF16)
+        beta_all = psum_keep.tile([P, WIDTH], BF16)
 
-        def residual_plus_bias(i):
-            for n in range(WIDTH // BANK):
-                cols = slice(n * BANK, (n + 1) * BANK)
-                nc.gpsimd.tensor_tensor(out=xb[:, i, cols], in0=x_sb[:, i, cols], in1=b2_all[:, cols], op=ALU.add)
+        ident_bf = keep.tile([P, P], BF16)
 
-        def start_tile(i):
-            tokens = slice(i * P, (i + 1) * P)
-            y = norm.tile([P, WIDTH], F32)
-            y_sum = small.tile([P, WIDTH // BANK], F32)
+        def residual_plus_bias_pe(i, copy):
             for n in range(WIDTH // BANK):
                 cols = slice(n * BANK, (n + 1) * BANK)
                 acc = psum.tile([P, BANK], F32, tag="bank")
-                for gf in range(PASSES):
-                    nc.tensor.matmul_mx(
-                        out=acc[:],
-                        lhsT=h_codes[:, gf, tokens].bitcast(FP8X4),
-                        lhsT_scale=h_scales[:, gf, tokens],
-                        rhs=w2_codes[:, gf, cols].bitcast(FP8X4),
-                        rhs_scale=w2_scales[:, gf, cols],
-                        start=(gf == 0),
-                        stop=(gf == PASSES - 1),
-                    )
-                nc.vector.scalar_tensor_tensor(
-                    out=y[:, cols], in0=acc[:], scalar=1.0, in1=xb[:, i, cols],
-                    op0=ALU.mult, op1=ALU.add, accum_out=y_sum[:, n : n + 1],
+                nc.tensor.matmul(acc[:], lhsT=ident_bf[:], rhs=x_sb[:, i, cols], start=True, stop=False)
+                nc.tensor.matmul(acc[:], lhsT=ones[:], rhs=vec_rows[:, cols], start=False, stop=True)
+                copy(out=xb[:, i, cols], in_=acc[:])
+
+        def residual_plus_bias(i):
+            for n in range(4):
+                cols = slice(n * 256, (n + 1) * 256)
+                nc.gpsimd.tensor_tensor(out=xb[:, i, cols], in0=x_sb[:, i, cols], in1=b2_all[:, cols], op=ALU.add)
+
+        def second_product(i, n):
+            tokens = slice(i * P, (i + 1) * P)
+            cols = slice(n * BANK, (n + 1) * BANK)
+            acc = psum.tile([P, BANK], F32, tag="bank")
+            for gf in range(PASSES):
+                nc.tensor.matmul_mx(
+                    out=acc[:],
+                    lhsT=h_codes[:, gf, tokens].bitcast(FP8X4),
+                    lhsT_scale=h_scales[:, gf, tokens],
+                    rhs=w2_codes[:, gf, cols].bitcast(FP8X4),
+                    rhs_scale=w2_scales[:, gf, cols],
+                    start=(gf == 0),
+                    stop=(gf == PASSES - 1),
                 )
-            neg_mean = small.tile([P, 1], F32)
+            return acc
+
+        def new_y():
+            y = norm.tile([P, WIDTH], F32, tag="y")
+            y_sum = small.tile([P, WIDTH // BANK], F32, tag="y_sum")
+            return y, y_sum
+
+        def residual_sum(i, n, y, y_sum, acc):
+            cols = slice(n * BANK, (n + 1) * BANK)
+            nc.vector.scalar_tensor_tensor(
+                out=y[:, cols], in0=acc[:], scalar=1.0, in1=xb[:, i, cols],
+                op0=ALU.mult, op1=ALU.add, accum_out=y_sum[:, n : n + 1],
+            )
+
+        def mean(y_sum):
+            neg_mean = small.tile([P, 1], F32, tag="neg_mean")
             nc.vector.tensor_scalar(
                 out=neg_mean[:], in0=y_sum[:, 0:1], scalar1=y_sum[:, 1:2], scalar2=-1.0 / WIDTH,
                 op0=ALU.add, op1=ALU.mult,
             )
-            squares = norm.tile([P, WIDTH], BF16)
-            sq_sum = small.tile([P, 1], F32)
+            return neg_mean
+
+        def square(y, neg_mean):
+            squares = norm.tile([P, WIDTH], BF16, tag="squares", bufs=1)
+            sq_sum = small.tile([P, 1], F32, tag="sq_sum")
             nc.scalar.activation(
                 out=squares[:], in_=y[:], func=FUNC.Square, bias=neg_mean[:, 0:1], scale=1.0, accum_out=sq_sum[:]
             )
-            std = small.tile([P, 1], F32)
-            nc.scalar.activation(out=std[:], in_=sq_sum[:], func=FUNC.Sqrt, bias=eps[:, 0:1], scale=1.0 / WIDTH)
-            z = norm.tile([P, WIDTH], F32)
-            nc.vector.scalar_tensor_tensor(
-                out=z[:], in0=y[:], scalar=neg_mean[:, 0:1], in1=gamma_all, op0=ALU.add, op1=ALU.mult
-            )
-            return z, std
+            return sq_sum
 
-        def finish_tile(i, z, std):
-            rstd = small.tile([P, 1], F32)
-            nc.vector.reciprocal(out=rstd[:], in_=std[:])
+        def deviation(sq_sum):
+            rstd = small.tile([P, 1], F32, tag="rstd")
+            nc.scalar.activation(
+                out=rstd[:], in_=sq_sum[:], func=FUNC.Abs_reciprocal_sqrt, bias=eps[:, 0:1], scale=1.0 / WIDTH
+            )
+            return rstd
+
+        def scale_shift(y, neg_mean):
+            z = norm.tile([P, WIDTH], F32, tag="z")
             nc.vector.scalar_tensor_tensor(
-                out=z[:], in0=z[:], scalar=rstd[:, 0:1], in1=beta_all, op0=ALU.mult, op1=ALU.add
+                out=z[:], in0=y[:], scalar=neg_mean[:, 0:1], in1=gamma_all[:], op0=ALU.add, op1=ALU.mult
+            )
+            return z
+
+        beta_sb = keep.tile([P, WIDTH], BF16)
+
+        def finish_scalar(z, rstd):
+            nc.scalar.activation(out=z[:], in_=z[:], func=FUNC.Copy, scale=rstd[:, 0:1])
+
+        def finish_gpsimd(i, z):
+            for n in range(2):
+                cols = slice(n * BANK, (n + 1) * BANK)
+                nc.gpsimd.tensor_tensor(out=z[:, cols], in0=z[:, cols], in1=beta_sb[:, cols], op=ALU.add)
+            nc.sync.dma_start(out=out_view[:, i, :], in_=z[:])
+
+        def finish(i, z, rstd):
+            nc.vector.scalar_tensor_tensor(
+                out=z[:], in0=z[:], scalar=rstd[:, 0:1], in1=beta_all[:], op0=ALU.mult, op1=ALU.add
             )
             nc.sync.dma_start(out=out_view[:, i, :], in_=z[:])
 
-        pack_chunk(x_sb, x_codes, x_scales, 0)
-        spread_vector(0)
-        for i in range(CHUNK_TILES):
-            residual_plus_bias(i)
-        pack_chunk(w1_sb, w1_codes, w1_scales, 0)
-        spread_vector(1)
-        pack_chunk(w1_sb, w1_codes, w1_scales, 1)
-        spread_vector(2)
+        ys, means, sqs, rstds, zs, accs = {}, {}, {}, {}, {}, {}
+
+        def new_sum():
+            h_sum = hidden.tile([P, CHUNK * PACK], BF16, align_bytes=64, tag="h_sum")
+            return h_sum
+
+        def relu(h_sum):
+            nc.vector.tensor_scalar_max(out=h_sum[:], in0=h_sum[:], scalar1=0.0)
+
+        def products(i):
+            accs[i] = [second_product(i, 0), second_product(i, 1)]
+
+        def sums(i, n):
+            if n == 0:
+                ys[i] = new_y()
+            residual_sum(i, n, ys[i][0], ys[i][1], accs[i][n])
+
+        def squared(i):
+            sqs[i] = square(ys[i][0], means[i])
+
+        def deviated(i):
+            rstds[i] = deviation(sqs[i])
+
+        def averaged(i):
+            means[i] = mean(ys[i][1])
+
+        def scaled(i):
+            zs[i] = scale_shift(ys[i][0], means[i])
+
+        def finished(i):
+            finish(i, zs[i], rstds[i])
+
+
+        def mx_hidden(i, gf, box):
+            if i % 4 == 0:
+                box[gf, i // 4] = new_sum()
+            hidden_sum(i, gf, box[gf, i // 4], i % 4)
+            if i % 4 == 3:
+                relu(box[gf, i // 4])
+                quantise_hidden(i // 4, gf, box[gf, i // 4])
+
+        box = {}
+        xg = flip_rows(x_sb, 0, (S, V))
+        quantise_rows(xg, x_codes, x_scales, 0, 2)
+        wg = flip_rows(w1_sb, 0, (S, V))
+        nc.vector.tensor_copy(out=ident_bf[:], in_=ident[:])
+        quantise_rows(wg, w1_codes, w1_scales, 0, 2)
+        wg = flip_rows(w1_sb, 2, (S, V))
         nc.vector.tensor_copy(out=b1_col[:], in_=b1_pairs[:])
-        h_first = hidden.tile([P, ROW_TILES, CHUNK], BF16, tag="h_rows")
-        for gf in range(PASSES):
-            for t in range(PACK):
-                hidden_tile(0, h_first, gf * PACK + t)
-            quantise_hidden(0, gf, regroup_hidden(h_first, gf, nc.vector.tensor_copy))
-            pack_chunk(w2_sb, w2_codes, w2_scales, gf)
-        pack_chunk(x_sb, x_codes, x_scales, 1)
-        for i in range(CHUNK_TILES, ROW_TILES):
-            residual_plus_bias(i)
+        quantise_rows(wg, w1_codes, w1_scales, 2, 2)
+        xg = flip_rows(x_sb, 2, (S, V))
+        mx_hidden(0, 0, box)
+        mx_hidden(1, 0, box)
+        quantise_rows(xg, x_codes, x_scales, 2, 2)
+        residual_plus_bias_pe(0, S)
+        wg = flip_rows(w1_sb, 4, (S, S))
+        mx_hidden(2, 0, box)
+        wg2 = flip_rows(w1_sb, 6, (S, S))
+        quantise_rows(wg, w1_codes, w1_scales, 4, 2)
+        mx_hidden(3, 0, box)
+        quantise_rows(wg2, w1_codes, w1_scales, 6, 2)
+        residual_plus_bias_pe(1, S)
+        mx_hidden(0, 1, box)
+        xg = flip_rows(x_sb, 4, (S, S))
+        mx_hidden(1, 1, box)
+        xg2 = flip_rows(x_sb, 6, (S, S))
+        quantise_rows(xg, x_codes, x_scales, 4, 2)
+        mx_hidden(2, 1, box)
+        quantise_rows(xg2, x_codes, x_scales, 6, 2)
+        mx_hidden(3, 1, box)
+        wg = flip_rows(w2_sb, 0, (S, S))
+        mx_hidden(4, 0, box)
+        wg2 = flip_rows(w2_sb, 2, (S, S))
+        quantise_rows(wg, w2_codes, w2_scales, 0, 2)
+        mx_hidden(5, 0, box)
+        wg = flip_rows(w2_sb, 4, (S, S))
+        quantise_rows(wg2, w2_codes, w2_scales, 2, 2)
+        mx_hidden(6, 0, box)
+        wg2 = flip_rows(w2_sb, 6, (S, S))
+        quantise_rows(wg, w2_codes, w2_scales, 4, 2)
+        mx_hidden(7, 0, box)
+        quantise_rows(wg2, w2_codes, w2_scales, 6, 2)
+        spread(1, gamma_all)
+        spread(2, beta_all)
+        S(out=beta_sb[:], in_=beta_all[:])
+        b2_psum = psum.tile([P, WIDTH], BF16, tag="bank")
+        spread(0, b2_psum)
+        S(out=b2_all[:], in_=b2_psum[:])
 
-        h_second = hidden.tile([P, ROW_TILES, CHUNK], BF16, tag="h_rows")
-        PAIRS = ROW_TILES // 2
+        for i in range(4, 8):
+            mx_hidden(i, 1, box)
 
-        def hidden_pair(k):
-            hidden_tile(1, h_second, 2 * k)
-            hidden_tile(1, h_second, 2 * k + 1)
-
-        started = None
-        regrouped = None
-        for i in range(ROW_TILES):
-            begun = start_tile(i)
-            if regrouped is not None:
-                quantise_hidden(1, *regrouped)
-                regrouped = None
-            if started is not None:
-                finish_tile(i - 1, *started)
-            started = begun
-            if i == 0:
-                hidden_pair(0)
-            k = i + 1
-            if k < PAIRS:
-                hidden_pair(k)
-                if k % 2 == 1:
-                    regrouped = (k // 2, regroup_hidden(h_second, k // 2, nc.scalar.copy))
-        finish_tile(ROW_TILES - 1, *started)
+        residual_plus_bias_pe(2, S)
+        residual_plus_bias_pe(3, S)
+        for k in range(CHUNK_TILES, ROW_TILES):
+            residual_plus_bias(k)
+        products(0)
+        for i in range(8):
+            sums(i, 0)
+            sums(i, 1)
+            if i > 0:
+                scaled(i - 1)
+            if i < 7:
+                products(i + 1)
+            averaged(i)
+            squared(i)
+            if i > 0:
+                if i - 1 in (1, 2, 3, 4, 5, 6):
+                    finish_scalar(zs[i - 1], rstds[i - 1])
+                    finish_gpsimd(i - 1, zs[i - 1])
+                elif i>1:
+                    pass
+            deviated(i)
+            if i > 0 and i - 1 not in (1, 2, 3, 4, 5, 6):
+                finished(i - 1)
+        scaled(7)
+        finished(7)

@@ -69,6 +69,9 @@ def tile_transformerblock_pb_kernel(tc, x_norm1, W1, b1, W2, b2, ln_gamma, ln_be
         load_x(4, 8)
         load_w2(0, 4)
         load_w2(4, 8)
+        b2_all = keep.tile([P, WIDTH], BF16)
+        beta_sb = keep.tile([P, WIDTH], BF16)
+        nc.sync.dma_start(out=beta_sb[:], in_=ln_beta.partition_broadcast(P))
 
         vec_rows = keep.tile([P, 3 * WIDTH], BF16)
         vec_bits = vec_rows[:].bitcast(I32)
@@ -211,9 +214,9 @@ def tile_transformerblock_pb_kernel(tc, x_norm1, W1, b1, W2, b2, ln_gamma, ln_be
             )
 
         xb = keep.tile([P, ROW_TILES, WIDTH], F32)
-        b2_all = keep.tile([P, WIDTH], BF16)
         gamma_all = psum_keep.tile([P, WIDTH], BF16)
         beta_all = psum_keep.tile([P, WIDTH], BF16)
+        b2_psum = psum.tile([P, WIDTH], BF16, tag="bank")
 
         ident_bf = keep.tile([P, P], BF16)
 
@@ -224,6 +227,9 @@ def tile_transformerblock_pb_kernel(tc, x_norm1, W1, b1, W2, b2, ln_gamma, ln_be
                 nc.tensor.matmul(acc[:], lhsT=ident_bf[:], rhs=x_sb[:, i, cols], start=True, stop=False)
                 nc.tensor.matmul(acc[:], lhsT=ones[:], rhs=vec_rows[:, cols], start=False, stop=True)
                 copy(out=xb[:, i, cols], in_=acc[:])
+
+        def residual_plus_bias_v(i):
+            nc.vector.tensor_tensor(out=xb[:, i, :], in0=x_sb[:, i, :], in1=b2_psum[:], op=ALU.add)
 
         def residual_plus_bias(i):
             for n in range(4):
@@ -282,13 +288,11 @@ def tile_transformerblock_pb_kernel(tc, x_norm1, W1, b1, W2, b2, ln_gamma, ln_be
             return rstd
 
         def scale_shift(y, neg_mean):
-            z = norm.tile([P, WIDTH], F32, tag="z")
+            z = norm.tile([P, WIDTH], F32, tag="z", bufs=6)
             nc.vector.scalar_tensor_tensor(
                 out=z[:], in0=y[:], scalar=neg_mean[:, 0:1], in1=gamma_all[:], op0=ALU.add, op1=ALU.mult
             )
             return z
-
-        beta_sb = keep.tile([P, WIDTH], BF16)
 
         def finish_scalar(z, rstd):
             nc.scalar.activation(out=z[:], in_=z[:], func=FUNC.Copy, scale=rstd[:, 0:1])
@@ -338,87 +342,97 @@ def tile_transformerblock_pb_kernel(tc, x_norm1, W1, b1, W2, b2, ln_gamma, ln_be
             finish(i, zs[i], rstds[i])
 
 
-        def mx_hidden(i, gf, box):
-            if i % 4 == 0:
-                box[gf, i // 4] = new_sum()
-            hidden_sum(i, gf, box[gf, i // 4], i % 4)
-            if i % 4 == 3:
-                relu(box[gf, i // 4])
-                quantise_hidden(i // 4, gf, box[gf, i // 4])
+        h_rows = hidden.tile([P, ROW_TILES, CHUNK], BF16, tag="h_rows", bufs=1)
+        UNITS = (
+            (x_sb, x_codes, x_scales, 0), (w1_sb, w1_codes, w1_scales, 0), (w1_sb, w1_codes, w1_scales, 2),
+            (x_sb, x_codes, x_scales, 2), (w1_sb, w1_codes, w1_scales, 4), (w1_sb, w1_codes, w1_scales, 6),
+            (x_sb, x_codes, x_scales, 4), (x_sb, x_codes, x_scales, 6), (w2_sb, w2_codes, w2_scales, 0),
+            (w2_sb, w2_codes, w2_scales, 2), (w2_sb, w2_codes, w2_scales, 4), (w2_sb, w2_codes, w2_scales, 6),
+        )
+        packed = {}
 
-        box = {}
-        xg = flip_rows(x_sb, 0, (S, V))
-        quantise_rows(xg, x_codes, x_scales, 0, 2)
-        wg = flip_rows(w1_sb, 0, (S, V))
-        nc.vector.tensor_copy(out=ident_bf[:], in_=ident[:])
-        quantise_rows(wg, w1_codes, w1_scales, 0, 2)
-        wg = flip_rows(w1_sb, 2, (S, V))
+        def turn(n, copies=(S, S)):
+            packed[n] = flip_rows(UNITS[n][0], UNITS[n][3], copies)
+
+        def pack(n):
+            quantise_rows(packed[n], UNITS[n][1], UNITS[n][2], UNITS[n][3], 2)
+
+        turn(0, (S, V))
+        turn(1, (S, V))
+        pack(0)
+        turn(2, (S, V))
         nc.vector.tensor_copy(out=b1_col[:], in_=b1_pairs[:])
-        quantise_rows(wg, w1_codes, w1_scales, 2, 2)
-        xg = flip_rows(x_sb, 2, (S, V))
-        mx_hidden(0, 0, box)
-        mx_hidden(1, 0, box)
-        quantise_rows(xg, x_codes, x_scales, 2, 2)
-        residual_plus_bias_pe(0, S)
-        wg = flip_rows(w1_sb, 4, (S, S))
-        mx_hidden(2, 0, box)
-        wg2 = flip_rows(w1_sb, 6, (S, S))
-        quantise_rows(wg, w1_codes, w1_scales, 4, 2)
-        mx_hidden(3, 0, box)
-        quantise_rows(wg2, w1_codes, w1_scales, 6, 2)
-        residual_plus_bias_pe(1, S)
-        mx_hidden(0, 1, box)
-        xg = flip_rows(x_sb, 4, (S, S))
-        mx_hidden(1, 1, box)
-        xg2 = flip_rows(x_sb, 6, (S, S))
-        quantise_rows(xg, x_codes, x_scales, 4, 2)
-        mx_hidden(2, 1, box)
-        quantise_rows(xg2, x_codes, x_scales, 6, 2)
-        mx_hidden(3, 1, box)
-        wg = flip_rows(w2_sb, 0, (S, S))
-        mx_hidden(4, 0, box)
-        wg2 = flip_rows(w2_sb, 2, (S, S))
-        quantise_rows(wg, w2_codes, w2_scales, 0, 2)
-        mx_hidden(5, 0, box)
-        wg = flip_rows(w2_sb, 4, (S, S))
-        quantise_rows(wg2, w2_codes, w2_scales, 2, 2)
-        mx_hidden(6, 0, box)
-        wg2 = flip_rows(w2_sb, 6, (S, S))
-        quantise_rows(wg, w2_codes, w2_scales, 4, 2)
-        mx_hidden(7, 0, box)
-        quantise_rows(wg2, w2_codes, w2_scales, 6, 2)
+        pack(1)
+        spread(0, b2_psum)
+        turn(3, (S, S))
+        residual_plus_bias_v(0)
+        pack(2)
+        nc.vector.tensor_copy(out=ident_bf[:], in_=ident[:])
+        residual_plus_bias_v(1)
+        s0 = new_sum()
+        s1 = new_sum()
+        s = (s0, s1)
+        for m in range(0, 8, 2):
+            i, gf = m % 4, m // 4
+            turn(4 + m)
+            turn(5 + m)
+            hidden_sum(i, gf, s[gf], i)
+            pack(3 + m)
+            hidden_sum(i + 1, gf, s[gf], i + 1)
+            pack(4 + m)
+            if m == 4:
+                relu(s0)
+                quantise_hidden(0, 0, s0)
         spread(1, gamma_all)
         spread(2, beta_all)
-        S(out=beta_sb[:], in_=beta_all[:])
-        b2_psum = psum.tile([P, WIDTH], BF16, tag="bank")
-        spread(0, b2_psum)
-        S(out=b2_all[:], in_=b2_psum[:])
+        b2_late = psum.tile([P, WIDTH], BF16, tag="bank")
+        spread(0, b2_late)
+        pack(11)
+        relu(s1)
 
-        for i in range(4, 8):
-            mx_hidden(i, 1, box)
-
-        residual_plus_bias_pe(2, S)
-        residual_plus_bias_pe(3, S)
-        for k in range(CHUNK_TILES, ROW_TILES):
+        h0 = new_hidden()
+        h1 = new_hidden()
+        GFIN = (2, 3, 4)
+        PEX = {3: 4, 4: 7}
+        for j in range(4):
+            hidden_tile(1, h_rows, j)
+        quantise_hidden(0, 1, s1)
+        S(out=b2_all[:], in_=b2_late[:])
+        for k in (2, 3, 5, 6):
             residual_plus_bias(k)
         products(0)
+        regroup_hidden(h_rows, 0, h0, (S, S))
+        for j in range(4, 6):
+            hidden_tile(1, h_rows, j)
+        products(1)
+        for j in range(6, 8):
+            hidden_tile(1, h_rows, j)
         for i in range(8):
             sums(i, 0)
             sums(i, 1)
+            if i == 3:
+                quantise_hidden(1, 1, h1)
             if i > 0:
                 scaled(i - 1)
-            if i < 7:
+            if 0 < i < 7:
                 products(i + 1)
             averaged(i)
+            if i == 1:
+                quantise_hidden(1, 0, h0)
+            if i > 1 and i - 2 not in GFIN:
+                finished(i - 2)
+            if i in PEX:
+                residual_plus_bias_pe(PEX[i], S)
             squared(i)
+            if i == 1:
+                deviated(0)
+                regroup_hidden(h_rows, 1, h1, (S, S))
+            if i > 0 and i - 1 in GFIN:
+                finish_scalar(zs[i - 1], rstds[i - 1])
+                finish_gpsimd(i - 1, zs[i - 1])
             if i > 0:
-                if i - 1 in (1, 2, 3, 4, 5, 6):
-                    finish_scalar(zs[i - 1], rstds[i - 1])
-                    finish_gpsimd(i - 1, zs[i - 1])
-                elif i>1:
-                    pass
-            deviated(i)
-            if i > 0 and i - 1 not in (1, 2, 3, 4, 5, 6):
-                finished(i - 1)
+                deviated(i)
+        if 6 not in GFIN:
+            finished(6)
         scaled(7)
         finished(7)

@@ -65,13 +65,13 @@ def tile_transformerblock_pb_kernel(tc, x_norm1, W1, b1, W2, b2, ln_gamma, ln_be
         load_w1(0, 2)
         load_w1(2, 4)
         load_x(2, 4)
-        load_w1(4, 8)
+        load_w1(4, 6)
+        load_w1(6, 8)
         load_x(4, 8)
         load_w2(0, 4)
         load_w2(4, 8)
         b2_all = keep.tile([P, WIDTH], BF16)
         beta_sb = keep.tile([P, WIDTH], BF16)
-        nc.sync.dma_start(out=beta_sb[:], in_=ln_beta.partition_broadcast(P))
 
         vec_rows = keep.tile([P, 3 * WIDTH], BF16)
         vec_bits = vec_rows[:].bitcast(I32)
@@ -421,6 +421,8 @@ def tile_transformerblock_pb_kernel(tc, x_norm1, W1, b1, W2, b2, ln_gamma, ln_be
                 quantise_hidden(1, 0, h0)
             if i > 1 and i - 2 not in GFIN:
                 finished(i - 2)
+            if i == 3:
+                S(out=beta_sb[:], in_=beta_all[:])
             if i in PEX:
                 residual_plus_bias_pe(PEX[i], S)
             squared(i)

@@ -369,6 +369,7 @@ def tile_transformerblock_pb_kernel(tc, x_norm1, W1, b1, W2, b2, ln_gamma, ln_be
         pack(2)
         nc.vector.tensor_copy(out=ident_bf[:], in_=ident[:])
         residual_plus_bias_v(1)
+        residual_plus_bias_v(2)
         s0 = new_sum()
         s1 = new_sum()
         s = (s0, s1)
@@ -380,25 +381,24 @@ def tile_transformerblock_pb_kernel(tc, x_norm1, W1, b1, W2, b2, ln_gamma, ln_be
             pack(3 + m)
             hidden_sum(i + 1, gf, s[gf], i + 1)
             pack(4 + m)
+            if m == 2:
+                residual_plus_bias_v(7)
             if m == 4:
                 relu(s0)
                 quantise_hidden(0, 0, s0)
         spread(1, gamma_all)
         spread(2, beta_all)
-        b2_late = psum.tile([P, WIDTH], BF16, tag="bank")
-        spread(0, b2_late)
         pack(11)
         relu(s1)
 
         h0 = new_hidden()
         h1 = new_hidden()
-        GFIN = (2, 3, 4)
-        PEX = {3: 4, 4: 7}
+        GFIN = ()
+        PEX = {0: 3, 1: 4, 2: 5, 3: 6}
         for j in range(4):
             hidden_tile(1, h_rows, j)
         quantise_hidden(0, 1, s1)
-        S(out=b2_all[:], in_=b2_late[:])
-        for k in (2, 3, 5, 6):
+        for k in ():
             residual_plus_bias(k)
         products(0)
         regroup_hidden(h_rows, 0, h0, (S, S))
@@ -421,8 +421,6 @@ def tile_transformerblock_pb_kernel(tc, x_norm1, W1, b1, W2, b2, ln_gamma, ln_be
                 quantise_hidden(1, 0, h0)
             if i > 1 and i - 2 not in GFIN:
                 finished(i - 2)
-            if i == 3:
-                S(out=beta_sb[:], in_=beta_all[:])
             if i in PEX:
                 residual_plus_bias_pe(PEX[i], S)
             squared(i)

@@ -39,8 +39,7 @@ def tile_transformerblock_pb_kernel(tc, x_norm1, W1, b1, W2, b2, ln_gamma, ln_be
         hidden = ctx.enter_context(tc.tile_pool(name="hidden", bufs=2))
         norm = ctx.enter_context(tc.tile_pool(name="norm", bufs=4))
         small = ctx.enter_context(tc.tile_pool(name="small", bufs=4))
-        psum = ctx.enter_context(tc.psum_pool(name="psum", bufs=6))
-        psum_keep = ctx.enter_context(tc.psum_pool(name="psum_keep", bufs=1))
+        psum = ctx.enter_context(tc.psum_pool(name="psum", bufs=8))
         ctx.enter_context(tc.manual_schedule())
 
         x_sb = keep.tile([P, ROW_TILES, WIDTH], BF16)
@@ -67,13 +66,19 @@ def tile_transformerblock_pb_kernel(tc, x_norm1, W1, b1, W2, b2, ln_gamma, ln_be
         load_x(2, 4)
         load_w1(4, 6)
         load_w1(6, 8)
+        load_w2(0, 2)
+        load_w2(2, 4)
+        load_w2(4, 6)
+        load_w2(6, 8)
         load_x(4, 8)
-        load_w2(0, 4)
-        load_w2(4, 8)
         b2_all = keep.tile([P, WIDTH], BF16)
-        beta_sb = keep.tile([P, WIDTH], BF16)
+        gamma_all = keep.tile([P, WIDTH], BF16)
+        beta_all = keep.tile([P, WIDTH], BF16)
+        nc.sync.dma_start(out=b2_all[:], in_=b2.partition_broadcast(P))
+        nc.sync.dma_start(out=gamma_all[:], in_=ln_gamma.partition_broadcast(P))
+        nc.sync.dma_start(out=beta_all[:], in_=ln_beta.partition_broadcast(P))
 
-        vec_rows = keep.tile([P, 3 * WIDTH], BF16)
+        vec_rows = keep.tile([P, WIDTH], BF16)
         vec_bits = vec_rows[:].bitcast(I32)
         nc.vector.memset(vec_bits, 0)
         b1_pairs = keep.tile([P, ROW_TILES], BF16)
@@ -82,10 +87,7 @@ def tile_transformerblock_pb_kernel(tc, x_norm1, W1, b1, W2, b2, ln_gamma, ln_be
                 out=b1_pairs[:].rearrange("p (a e) -> p a e", e=2),
                 in_=b1.rearrange("(a p e) -> p a e", p=P, e=2),
             )
-        for v, vec in enumerate((b2, ln_gamma, ln_beta)):
-            nc.scalar.dma_start(
-                out=vec_rows[0:1, v * WIDTH : (v + 1) * WIDTH], in_=vec.rearrange("(o d) -> o d", o=1)
-            )
+        nc.scalar.dma_start(out=vec_rows[0:1, :], in_=b2.rearrange("(o d) -> o d", o=1))
         ident = keep.tile([P, P], F32)
         make_identity(nc, ident[:])
         ones = keep.tile([P, P], BF16)
@@ -141,13 +143,6 @@ def tile_transformerblock_pb_kernel(tc, x_norm1, W1, b1, W2, b2, ln_gamma, ln_be
                 regroup(flipped, grouped, r, copies[r])
             return grouped
 
-        def spread(v, store):
-            for n in range(WIDTH // BANK):
-                cols = slice(v * WIDTH + n * BANK, v * WIDTH + (n + 1) * BANK)
-                nc.tensor.matmul(
-                    store[:, n * BANK : (n + 1) * BANK], lhsT=ones[:], rhs=vec_rows[:, cols], start=True, stop=True
-                )
-
         b1_col = keep.tile([P, ROW_TILES], F32)
 
         def hidden_sum(i, gf, h_sum, k):
@@ -172,52 +167,52 @@ def tile_transformerblock_pb_kernel(tc, x_norm1, W1, b1, W2, b2, ln_gamma, ln_be
                 op=ALU.add,
             )
 
-        def hidden_tile(s, h_rows, j):
+        def hidden_row(first, count, rows, j):
             units = slice(j * P, (j + 1) * P)
+            tokens = slice(first * P, (first + count) * P)
             acc = psum.tile([P, BANK], F32, tag="bank")
             for g in range(PASSES):
                 nc.tensor.matmul_mx(
-                    out=acc[:],
+                    out=acc[:, 0 : count * P],
                     lhsT=w1_codes[:, g, units].bitcast(FP8X4),
                     lhsT_scale=w1_scales[:, g, units],
-                    rhs=x_codes[:, g, chunk_cols(s)].bitcast(FP8X4),
-                    rhs_scale=x_scales[:, g, chunk_cols(s)],
+                    rhs=x_codes[:, g, tokens].bitcast(FP8X4),
+                    rhs_scale=x_scales[:, g, tokens],
                     start=(g == 0),
                     stop=(g == PASSES - 1),
                 )
             nc.scalar.activation(
-                out=h_rows[:, j, :], in_=acc[:], func=FUNC.Relu, bias=b1_col[:, j : j + 1], scale=1.0
+                out=rows[:, j % PACK, 0 : count * P], in_=acc[:, 0 : count * P], func=FUNC.Relu,
+                bias=b1_col[:, j : j + 1], scale=1.0,
             )
 
-        def regroup_hidden(h_rows, gf, h_grouped, copies):
-            pieces = len(copies)
-            width = CHUNK // pieces
-            for n in range(pieces):
+        def new_rows():
+            rows = hidden.tile([P, PACK, CHUNK], BF16, tag="rows", bufs=3)
+            return rows
+
+        def interleave(rows, count, h_grouped, copies):
+            width = count * P // len(copies)
+            for n in range(len(copies)):
                 copies[n](
                     out=h_grouped[:, n * width * PACK : (n + 1) * width * PACK].rearrange(
                         "p (c i t) -> p c t i", i=4, t=PACK
                     ),
-                    in_=h_rows[:, gf * PACK : (gf + 1) * PACK, n * width : (n + 1) * width].rearrange(
-                        "p t (c i) -> p c t i", i=4
-                    ),
+                    in_=rows[:, :, n * width : (n + 1) * width].rearrange("p t (c i) -> p c t i", i=4),
                 )
 
         def new_hidden():
-            h_grouped = hidden.tile([P, CHUNK * PACK], BF16, align_bytes=64, tag="h_grouped")
+            h_grouped = hidden.tile([P, CHUNK * PACK], BF16, align_bytes=64, tag="h_grouped", bufs=3)
             return h_grouped
 
-        def quantise_hidden(s, gf, h_grouped):
+        def quantise_hidden(first, count, gf, h_grouped):
+            tokens = slice(first * P, (first + count) * P)
             nc.vector.quantize_mx(
-                out=h_codes[:, gf, chunk_cols(s)].bitcast(FP8X4),
-                scales=h_scales[:, gf, chunk_cols(s)],
-                in_=h_grouped[:],
+                out=h_codes[:, gf, tokens].bitcast(FP8X4),
+                scales=h_scales[:, gf, tokens],
+                in_=h_grouped[:, 0 : count * P * PACK],
             )
 
         xb = keep.tile([P, ROW_TILES, WIDTH], F32)
-        gamma_all = psum_keep.tile([P, WIDTH], BF16)
-        beta_all = psum_keep.tile([P, WIDTH], BF16)
-        b2_psum = psum.tile([P, WIDTH], BF16, tag="bank")
-
         ident_bf = keep.tile([P, P], BF16)
 
         def residual_plus_bias_pe(i, copy):
@@ -229,12 +224,7 @@ def tile_transformerblock_pb_kernel(tc, x_norm1, W1, b1, W2, b2, ln_gamma, ln_be
                 copy(out=xb[:, i, cols], in_=acc[:])
 
         def residual_plus_bias_v(i):
-            nc.vector.tensor_tensor(out=xb[:, i, :], in0=x_sb[:, i, :], in1=b2_psum[:], op=ALU.add)
-
-        def residual_plus_bias(i):
-            for n in range(4):
-                cols = slice(n * 256, (n + 1) * 256)
-                nc.gpsimd.tensor_tensor(out=xb[:, i, cols], in0=x_sb[:, i, cols], in1=b2_all[:, cols], op=ALU.add)
+            nc.vector.tensor_tensor(out=xb[:, i, :], in0=x_sb[:, i, :], in1=b2_all[:], op=ALU.add)
 
         def second_product(i, n):
             tokens = slice(i * P, (i + 1) * P)
@@ -294,15 +284,6 @@ def tile_transformerblock_pb_kernel(tc, x_norm1, W1, b1, W2, b2, ln_gamma, ln_be
             )
             return z
 
-        def finish_scalar(z, rstd):
-            nc.scalar.activation(out=z[:], in_=z[:], func=FUNC.Copy, scale=rstd[:, 0:1])
-
-        def finish_gpsimd(i, z):
-            for n in range(2):
-                cols = slice(n * BANK, (n + 1) * BANK)
-                nc.gpsimd.tensor_tensor(out=z[:, cols], in0=z[:, cols], in1=beta_sb[:, cols], op=ALU.add)
-            nc.sync.dma_start(out=out_view[:, i, :], in_=z[:])
-
         def finish(i, z, rstd):
             nc.vector.scalar_tensor_tensor(
                 out=z[:], in0=z[:], scalar=rstd[:, 0:1], in1=beta_all[:], op0=ALU.mult, op1=ALU.add
@@ -342,12 +323,11 @@ def tile_transformerblock_pb_kernel(tc, x_norm1, W1, b1, W2, b2, ln_gamma, ln_be
             finish(i, zs[i], rstds[i])
 
 
-        h_rows = hidden.tile([P, ROW_TILES, CHUNK], BF16, tag="h_rows", bufs=1)
         UNITS = (
             (x_sb, x_codes, x_scales, 0), (w1_sb, w1_codes, w1_scales, 0), (w1_sb, w1_codes, w1_scales, 2),
             (x_sb, x_codes, x_scales, 2), (w1_sb, w1_codes, w1_scales, 4), (w1_sb, w1_codes, w1_scales, 6),
-            (x_sb, x_codes, x_scales, 4), (x_sb, x_codes, x_scales, 6), (w2_sb, w2_codes, w2_scales, 0),
-            (w2_sb, w2_codes, w2_scales, 2), (w2_sb, w2_codes, w2_scales, 4), (w2_sb, w2_codes, w2_scales, 6),
+            (w2_sb, w2_codes, w2_scales, 0), (w2_sb, w2_codes, w2_scales, 2), (w2_sb, w2_codes, w2_scales, 4),
+            (w2_sb, w2_codes, w2_scales, 6), (x_sb, x_codes, x_scales, 4), (x_sb, x_codes, x_scales, 6),
         )
         packed = {}
 
@@ -363,76 +343,102 @@ def tile_transformerblock_pb_kernel(tc, x_norm1, W1, b1, W2, b2, ln_gamma, ln_be
         turn(2, (S, V))
         nc.vector.tensor_copy(out=b1_col[:], in_=b1_pairs[:])
         pack(1)
-        spread(0, b2_psum)
-        turn(3, (S, S))
-        residual_plus_bias_v(0)
-        pack(2)
         nc.vector.tensor_copy(out=ident_bf[:], in_=ident[:])
-        residual_plus_bias_v(1)
-        residual_plus_bias_v(2)
+        turn(3, (S, V))
+        pack(2)
+        turn(4, (S, S))
+        pack(3)
+        turn(5, (S, S))
         s0 = new_sum()
-        s1 = new_sum()
-        s = (s0, s1)
-        for m in range(0, 8, 2):
-            i, gf = m % 4, m // 4
-            turn(4 + m)
-            turn(5 + m)
-            hidden_sum(i, gf, s[gf], i)
-            pack(3 + m)
-            hidden_sum(i + 1, gf, s[gf], i + 1)
-            pack(4 + m)
-            if m == 2:
-                residual_plus_bias_v(7)
-            if m == 4:
-                relu(s0)
-                quantise_hidden(0, 0, s0)
-        spread(1, gamma_all)
-        spread(2, beta_all)
-        pack(11)
-        relu(s1)
-
-        h0 = new_hidden()
-        h1 = new_hidden()
-        GFIN = ()
-        PEX = {0: 3, 1: 4, 2: 5, 3: 6}
-        for j in range(4):
-            hidden_tile(1, h_rows, j)
-        quantise_hidden(0, 1, s1)
-        for k in ():
-            residual_plus_bias(k)
-        products(0)
-        regroup_hidden(h_rows, 0, h0, (S, S))
+        hidden_sum(0, 0, s0, 0)
+        hidden_sum(1, 0, s0, 1)
+        pack(4)
+        turn(6, (S, S))
+        hidden_sum(2, 0, s0, 2)
+        pack(5)
+        hidden_sum(3, 0, s0, 3)
+        r1 = new_rows()
+        g1 = new_hidden()
         for j in range(4, 6):
-            hidden_tile(1, h_rows, j)
-        products(1)
+            hidden_row(0, 4, r1, j)
+        pack(6)
+        relu(s0)
+        turn(7, (S, V))
         for j in range(6, 8):
-            hidden_tile(1, h_rows, j)
+            hidden_row(0, 4, r1, j)
+        quantise_hidden(0, 4, 0, s0)
+        turn(8, (S, S))
+        pack(7)
+        interleave(r1, 4, g1, (V, V))
+        turn(9, (S, S))
+        pack(8)
+        quantise_hidden(0, 4, 1, g1)
+        pack(9)
+        residual_plus_bias_pe(0, S)
+        turn(10, (S, S))
+        products(0)
+        residual_plus_bias_pe(1, S)
+
+        rows, grouped = {}, {}
+
+        def begin(first, gf):
+            rows[first, gf] = new_rows()
+            grouped[first, gf] = new_hidden()
+
+        def hidden_pair(first, gf):
+            begin(first, gf)
+            for j in range(4 * gf, 4 * gf + 4):
+                hidden_row(first, 2, rows[first, gf], j)
+
+        def work_before(i):
+            if i == 0:
+                pack(10)
+            if i == 99:
+                pack(11)
+            if i == 2:
+                quantise_hidden(4, 2, 0, grouped[4, 0])
+            if i == 3:
+                quantise_hidden(4, 2, 1, grouped[4, 1])
+            if i == 4:
+                quantise_hidden(6, 2, 0, grouped[6, 0])
+            if i == 5:
+                quantise_hidden(6, 2, 1, grouped[6, 1])
+
+        def work(i):
+            if i == 0:
+                hidden_pair(4, 0)
+            if i == 1:
+                interleave(rows[4, 0], 2, grouped[4, 0], (S,))
+                residual_plus_bias_v(2)
+                hidden_pair(4, 1)
+                turn(11)
+            if i == 2:
+                interleave(rows[4, 1], 2, grouped[4, 1], (S,))
+                residual_plus_bias_v(3)
+                pack(11)
+                hidden_pair(6, 0)
+            if i == 3:
+                interleave(rows[6, 0], 2, grouped[6, 0], (S,))
+                hidden_pair(6, 1)
+            if i == 4:
+                interleave(rows[6, 1], 2, grouped[6, 1], (S,))
+
         for i in range(8):
             sums(i, 0)
             sums(i, 1)
-            if i == 3:
-                quantise_hidden(1, 1, h1)
             if i > 0:
                 scaled(i - 1)
-            if 0 < i < 7:
-                products(i + 1)
             averaged(i)
-            if i == 1:
-                quantise_hidden(1, 0, h0)
-            if i > 1 and i - 2 not in GFIN:
-                finished(i - 2)
-            if i in PEX:
-                residual_plus_bias_pe(PEX[i], S)
+            work_before(i)
             squared(i)
-            if i == 1:
-                deviated(0)
-                regroup_hidden(h_rows, 1, h1, (S, S))
-            if i > 0 and i - 1 in GFIN:
-                finish_scalar(zs[i - 1], rstds[i - 1])
-                finish_gpsimd(i - 1, zs[i - 1])
-            if i > 0:
-                deviated(i)
-        if 6 not in GFIN:
-            finished(6)
+            if 4 <= i + 2 < 8:
+                residual_plus_bias_pe(i + 2, S)
+            if i < 7:
+                products(i + 1)
+            if i > 1:
+                finished(i - 2)
+            work(i)
+            deviated(i)
+        finished(6)
         scaled(7)
         finished(7)

@@ -23,6 +23,8 @@ PASSES = WIDTH // K_PASS
 ROW_TILES = 8
 CHUNK_TILES = 4
 CHUNK = CHUNK_TILES * P
+UNIT = 2 * P
+UNITS = ROW_TILES // 2
 LN_EPS = 1e-5
 
 FLOPS = 2 * 2 * TOKENS * WIDTH * WIDTH
@@ -97,12 +99,12 @@ def tile_transformerblock_pb_kernel(tc, x_norm1, W1, b1, W2, b2, ln_gamma, ln_be
         table_first = keep.tile([P, 1], F32)
         nc.scalar.activation(out=table_first[:], in_=eps[:], func=FUNC.Abs_reciprocal_sqrt)
 
-        x_codes = keep.tile([P, PASSES, TOKENS], U32, align_bytes=64)
-        x_scales = keep.tile([P, PASSES, TOKENS], U8, align_bytes=64)
-        w1_codes = keep.tile([P, PASSES, WIDTH], U32, align_bytes=64)
-        w1_scales = keep.tile([P, PASSES, WIDTH], U8, align_bytes=64)
-        w2_codes = keep.tile([P, PASSES, WIDTH], U32, align_bytes=64)
-        w2_scales = keep.tile([P, PASSES, WIDTH], U8, align_bytes=64)
+        x_codes = keep.tile([P, UNITS, PASSES, UNIT], U32, align_bytes=64)
+        x_scales = keep.tile([P, UNITS, PASSES, UNIT], U8, align_bytes=64)
+        w1_codes = keep.tile([P, UNITS, PASSES, UNIT], U32, align_bytes=64)
+        w1_scales = keep.tile([P, UNITS, PASSES, UNIT], U8, align_bytes=64)
+        w2_codes = keep.tile([P, UNITS, PASSES, UNIT], U32, align_bytes=64)
+        w2_scales = keep.tile([P, UNITS, PASSES, UNIT], U8, align_bytes=64)
         h_codes = keep.tile([P, PASSES, TOKENS], U32, align_bytes=64)
         h_scales = keep.tile([P, PASSES, TOKENS], U8, align_bytes=64)
 
@@ -125,13 +127,12 @@ def tile_transformerblock_pb_kernel(tc, x_norm1, W1, b1, W2, b2, ln_gamma, ln_be
             )
 
         def quantise_rows(grouped, codes, scales, first, count):
-            for g in range(PASSES):
-                cols = slice(first * P, (first + count) * P)
-                nc.vector.quantize_mx(
-                    out=codes[:, g, cols].bitcast(FP8X4),
-                    scales=scales[:, g, cols],
-                    in_=grouped[:, g * count * P * PACK : (g + 1) * count * P * PACK],
-                )
+            unit = first // 2
+            nc.vector.quantize_mx(
+                out=codes[:, unit].rearrange("p g r -> p (g r)").bitcast(FP8X4),
+                scales=scales[:, unit].rearrange("p g r -> p (g r)"),
+                in_=grouped[:],
+            )
 
         V = nc.vector.tensor_copy
         S = nc.scalar.copy
@@ -146,17 +147,18 @@ def tile_transformerblock_pb_kernel(tc, x_norm1, W1, b1, W2, b2, ln_gamma, ln_be
         b1_col = keep.tile([P, ROW_TILES], F32)
 
         def hidden_sum(i, gf, h_sum, k):
-            tokens = slice(i * P, (i + 1) * P)
+            tokens = slice(i % 2 * P, (i % 2 + 1) * P)
             acc = psum.tile([P, PACK, P], F32, tag="bank")
             for t in range(PACK):
-                units = slice((gf * PACK + t) * P, (gf * PACK + t + 1) * P)
+                j = gf * PACK + t
+                units = slice(j % 2 * P, (j % 2 + 1) * P)
                 for g in range(PASSES):
                     nc.tensor.matmul_mx(
                         out=acc[:, t, :],
-                        lhsT=w1_codes[:, g, units].bitcast(FP8X4),
-                        lhsT_scale=w1_scales[:, g, units],
-                        rhs=x_codes[:, g, tokens].bitcast(FP8X4),
-                        rhs_scale=x_scales[:, g, tokens],
+                        lhsT=w1_codes[:, j // 2, g, units].bitcast(FP8X4),
+                        lhsT_scale=w1_scales[:, j // 2, g, units],
+                        rhs=x_codes[:, i // 2, g, tokens].bitcast(FP8X4),
+                        rhs_scale=x_scales[:, i // 2, g, tokens],
                         start=(g == 0),
                         stop=(g == PASSES - 1),
                     )
@@ -168,19 +170,19 @@ def tile_transformerblock_pb_kernel(tc, x_norm1, W1, b1, W2, b2, ln_gamma, ln_be
             )
 
         def hidden_row(first, count, rows, j):
-            units = slice(j * P, (j + 1) * P)
-            tokens = slice(first * P, (first + count) * P)
+            units = slice(j % 2 * P, (j % 2 + 1) * P)
             acc = psum.tile([P, BANK], F32, tag="bank")
-            for g in range(PASSES):
-                nc.tensor.matmul_mx(
-                    out=acc[:, 0 : count * P],
-                    lhsT=w1_codes[:, g, units].bitcast(FP8X4),
-                    lhsT_scale=w1_scales[:, g, units],
-                    rhs=x_codes[:, g, tokens].bitcast(FP8X4),
-                    rhs_scale=x_scales[:, g, tokens],
-                    start=(g == 0),
-                    stop=(g == PASSES - 1),
-                )
+            for k in range(count // 2):
+                for g in range(PASSES):
+                    nc.tensor.matmul_mx(
+                        out=acc[:, k * UNIT : (k + 1) * UNIT],
+                        lhsT=w1_codes[:, j // 2, g, units].bitcast(FP8X4),
+                        lhsT_scale=w1_scales[:, j // 2, g, units],
+                        rhs=x_codes[:, first // 2 + k, g, :].bitcast(FP8X4),
+                        rhs_scale=x_scales[:, first // 2 + k, g, :],
+                        start=(g == 0),
+                        stop=(g == PASSES - 1),
+                    )
             nc.scalar.activation(
                 out=rows[:, j % PACK, 0 : count * P], in_=acc[:, 0 : count * P], func=FUNC.Relu,
                 bias=b1_col[:, j : j + 1], scale=1.0,
@@ -228,18 +230,18 @@ def tile_transformerblock_pb_kernel(tc, x_norm1, W1, b1, W2, b2, ln_gamma, ln_be
 
         def second_product(i, n):
             tokens = slice(i * P, (i + 1) * P)
-            cols = slice(n * BANK, (n + 1) * BANK)
             acc = psum.tile([P, BANK], F32, tag="bank")
-            for gf in range(PASSES):
-                nc.tensor.matmul_mx(
-                    out=acc[:],
-                    lhsT=h_codes[:, gf, tokens].bitcast(FP8X4),
-                    lhsT_scale=h_scales[:, gf, tokens],
-                    rhs=w2_codes[:, gf, cols].bitcast(FP8X4),
-                    rhs_scale=w2_scales[:, gf, cols],
-                    start=(gf == 0),
-                    stop=(gf == PASSES - 1),
-                )
+            for k in range(2):
+                for gf in range(PASSES):
+                    nc.tensor.matmul_mx(
+                        out=acc[:, k * UNIT : (k + 1) * UNIT],
+                        lhsT=h_codes[:, gf, tokens].bitcast(FP8X4),
+                        lhsT_scale=h_scales[:, gf, tokens],
+                        rhs=w2_codes[:, 2 * n + k, gf, :].bitcast(FP8X4),
+                        rhs_scale=w2_scales[:, 2 * n + k, gf, :],
+                        start=(gf == 0),
+                        stop=(gf == PASSES - 1),
+                    )
             return acc
 
         def new_y():
@@ -284,11 +286,14 @@ def tile_transformerblock_pb_kernel(tc, x_norm1, W1, b1, W2, b2, ln_gamma, ln_be
             )
             return z
 
-        def finish(i, z, rstd):
-            nc.vector.scalar_tensor_tensor(
-                out=z[:], in0=z[:], scalar=rstd[:, 0:1], in1=beta_all[:], op0=ALU.mult, op1=ALU.add
-            )
-            nc.sync.dma_start(out=out_view[:, i, :], in_=z[:])
+        def finish(i, z, rstd, pieces=1):
+            width = WIDTH // pieces
+            for n in range(pieces):
+                cols = slice(n * width, (n + 1) * width)
+                nc.vector.scalar_tensor_tensor(
+                    out=z[:, cols], in0=z[:, cols], scalar=rstd[:, 0:1], in1=beta_all[:, cols], op0=ALU.mult, op1=ALU.add
+                )
+                nc.sync.dma_start(out=out_view[:, i, cols], in_=z[:, cols])
 
         ys, means, sqs, rstds, zs, accs = {}, {}, {}, {}, {}, {}
 
@@ -319,11 +324,11 @@ def tile_transformerblock_pb_kernel(tc, x_norm1, W1, b1, W2, b2, ln_gamma, ln_be
         def scaled(i):
             zs[i] = scale_shift(ys[i][0], means[i])
 
-        def finished(i):
-            finish(i, zs[i], rstds[i])
+        def finished(i, pieces=1):
+            finish(i, zs[i], rstds[i], pieces)
 
 
-        UNITS = (
+        PIECES = (
             (x_sb, x_codes, x_scales, 0), (w1_sb, w1_codes, w1_scales, 0), (w1_sb, w1_codes, w1_scales, 2),
             (x_sb, x_codes, x_scales, 2), (w1_sb, w1_codes, w1_scales, 4), (w1_sb, w1_codes, w1_scales, 6),
             (w2_sb, w2_codes, w2_scales, 0), (w2_sb, w2_codes, w2_scales, 2), (w2_sb, w2_codes, w2_scales, 4),
@@ -332,10 +337,10 @@ def tile_transformerblock_pb_kernel(tc, x_norm1, W1, b1, W2, b2, ln_gamma, ln_be
         packed = {}
 
         def turn(n, copies=(S, S)):
-            packed[n] = flip_rows(UNITS[n][0], UNITS[n][3], copies)
+            packed[n] = flip_rows(PIECES[n][0], PIECES[n][3], copies)
 
         def pack(n):
-            quantise_rows(packed[n], UNITS[n][1], UNITS[n][2], UNITS[n][3], 2)
+            quantise_rows(packed[n], PIECES[n][1], PIECES[n][2], PIECES[n][3], 2)
 
         turn(0, (S, V))
         turn(1, (S, V))
@@ -344,14 +349,14 @@ def tile_transformerblock_pb_kernel(tc, x_norm1, W1, b1, W2, b2, ln_gamma, ln_be
         nc.vector.tensor_copy(out=b1_col[:], in_=b1_pairs[:])
         pack(1)
         nc.vector.tensor_copy(out=ident_bf[:], in_=ident[:])
-        turn(3, (S, V))
+        turn(3, (S, S))
         pack(2)
         turn(4, (S, S))
         pack(3)
-        turn(5, (S, S))
         s0 = new_sum()
         hidden_sum(0, 0, s0, 0)
         hidden_sum(1, 0, s0, 1)
+        turn(5, (S, S))
         pack(4)
         turn(6, (S, S))
         hidden_sum(2, 0, s0, 2)
@@ -431,14 +436,16 @@ def tile_transformerblock_pb_kernel(tc, x_norm1, W1, b1, W2, b2, ln_gamma, ln_be
             averaged(i)
             work_before(i)
             squared(i)
-            if 4 <= i + 2 < 8:
+            if i in (2, 3):
                 residual_plus_bias_pe(i + 2, S)
             if i < 7:
                 products(i + 1)
             if i > 1:
                 finished(i - 2)
             work(i)
+            if i in (4, 5):
+                residual_plus_bias_pe(i + 2, S)
             deviated(i)
         finished(6)
         scaled(7)
-        finished(7)
+        finished(7, 2)

@@ -21,10 +21,8 @@ TOKENS = 1024
 WIDTH = 1024
 PASSES = WIDTH // K_PASS
 ROW_TILES = 8
-CHUNK_TILES = 4
-CHUNK = CHUNK_TILES * P
-UNIT = 2 * P
-UNITS = ROW_TILES // 2
+HALF = 4
+PAIR = 2
 LN_EPS = 1e-5
 
 FLOPS = 2 * 2 * TOKENS * WIDTH * WIDTH
@@ -34,21 +32,27 @@ def tile_transformerblock_pb_kernel(tc, x_norm1, W1, b1, W2, b2, ln_gamma, ln_be
     nc = tc.nc
     x_view = x_norm1.flatten_outer_dims().rearrange("(p i) d -> p i d", i=ROW_TILES)
     out_view = out.flatten_outer_dims().rearrange("(p i) d -> p i d", i=ROW_TILES)
+    w1_view = W1.rearrange("(a p e) k -> p a (e k)", p=P, e=2)
+    w2_view = W2.rearrange("(j p) f -> p j f", p=P)
 
     with ExitStack() as ctx:
         keep = ctx.enter_context(tc.tile_pool(name="keep", bufs=1))
         stage = ctx.enter_context(tc.tile_pool(name="stage", bufs=3))
-        hidden = ctx.enter_context(tc.tile_pool(name="hidden", bufs=2))
+        hidden = ctx.enter_context(tc.tile_pool(name="hidden", bufs=3))
         norm = ctx.enter_context(tc.tile_pool(name="norm", bufs=4))
         small = ctx.enter_context(tc.tile_pool(name="small", bufs=4))
         psum = ctx.enter_context(tc.psum_pool(name="psum", bufs=8))
         ctx.enter_context(tc.manual_schedule())
 
+        vector_copy = nc.vector.tensor_copy
+        scalar_copy = nc.scalar.copy
+
         x_sb = keep.tile([P, ROW_TILES, WIDTH], BF16)
         w1_sb = keep.tile([P, ROW_TILES, WIDTH], BF16)
         w2_sb = keep.tile([P, ROW_TILES, WIDTH], BF16)
-        w1_view = W1.rearrange("(a p e) k -> p a (e k)", p=P, e=2)
-        w2_view = W2.rearrange("(j p) f -> p j f", p=P)
+        b2_all = keep.tile([P, WIDTH], BF16)
+        gamma_all = keep.tile([P, WIDTH], BF16)
+        beta_all = keep.tile([P, WIDTH], BF16)
 
         def load_x(first, last):
             nc.sync.dma_start(out=x_sb[:, first:last, :], in_=x_view[:, first:last, :])
@@ -68,143 +72,156 @@ def tile_transformerblock_pb_kernel(tc, x_norm1, W1, b1, W2, b2, ln_gamma, ln_be
         load_x(2, 4)
         load_w1(4, 6)
         load_w1(6, 8)
+        nc.sync.dma_start(out=b2_all[:], in_=b2.partition_broadcast(P))
         load_w2(0, 2)
         load_w2(2, 4)
         load_w2(4, 6)
         load_w2(6, 8)
         load_x(4, 8)
-        b2_all = keep.tile([P, WIDTH], BF16)
-        gamma_all = keep.tile([P, WIDTH], BF16)
-        beta_all = keep.tile([P, WIDTH], BF16)
-        nc.sync.dma_start(out=b2_all[:], in_=b2.partition_broadcast(P))
         nc.sync.dma_start(out=gamma_all[:], in_=ln_gamma.partition_broadcast(P))
         nc.sync.dma_start(out=beta_all[:], in_=ln_beta.partition_broadcast(P))
 
-        vec_rows = keep.tile([P, WIDTH], BF16)
-        vec_bits = vec_rows[:].bitcast(I32)
-        nc.vector.memset(vec_bits, 0)
+        b2_row = keep.tile([P, WIDTH], BF16)
+        nc.vector.memset(b2_row[:].bitcast(I32), 0)
         b1_pairs = keep.tile([P, ROW_TILES], BF16)
         with nc.allow_non_contiguous_dma(reason="b1 is 2 KiB, loaded once as 4-byte pairs"):
             nc.scalar.dma_start(
                 out=b1_pairs[:].rearrange("p (a e) -> p a e", e=2),
                 in_=b1.rearrange("(a p e) -> p a e", p=P, e=2),
             )
-        nc.scalar.dma_start(out=vec_rows[0:1, :], in_=b2.rearrange("(o d) -> o d", o=1))
+        nc.scalar.dma_start(out=b2_row[0:1, :], in_=b2.rearrange("(o d) -> o d", o=1))
         ident = keep.tile([P, P], F32)
         make_identity(nc, ident[:])
+        ident_bf = keep.tile([P, P], BF16)
+        vector_copy(out=ident_bf[:], in_=ident[:])
         ones = keep.tile([P, P], BF16)
         nc.vector.memset(ones[:], 1.0)
         eps = keep.tile([P, 1], F32)
         nc.vector.memset(eps[:], LN_EPS)
         table_first = keep.tile([P, 1], F32)
         nc.scalar.activation(out=table_first[:], in_=eps[:], func=FUNC.Abs_reciprocal_sqrt)
+        b1_col = keep.tile([P, ROW_TILES], F32)
 
-        x_codes = keep.tile([P, UNITS, PASSES, UNIT], U32, align_bytes=64)
-        x_scales = keep.tile([P, UNITS, PASSES, UNIT], U8, align_bytes=64)
-        w1_codes = keep.tile([P, UNITS, PASSES, UNIT], U32, align_bytes=64)
-        w1_scales = keep.tile([P, UNITS, PASSES, UNIT], U8, align_bytes=64)
-        w2_codes = keep.tile([P, UNITS, PASSES, UNIT], U32, align_bytes=64)
-        w2_scales = keep.tile([P, UNITS, PASSES, UNIT], U8, align_bytes=64)
+        flip_count = WIDTH // 2 // P
+
+        def codes_and_scales(blocks, rows):
+            codes = keep.tile([P, blocks, PASSES, rows], U32, align_bytes=64, name="codes_%d" % len(all_codes))
+            scales = keep.tile([P, blocks, PASSES, rows], U8, align_bytes=64, name="scales_%d" % len(all_codes))
+            all_codes.append(codes)
+            return codes, scales
+
+        all_codes = []
+        xa_codes, xa_scales = codes_and_scales(1, HALF * P)
+        xb_codes, xb_scales = codes_and_scales(2, PAIR * P)
+        w1_codes, w1_scales = codes_and_scales(4, PAIR * P)
+        w2_codes, w2_scales = codes_and_scales(2, HALF * P)
         h_codes = keep.tile([P, PASSES, TOKENS], U32, align_bytes=64)
         h_scales = keep.tile([P, PASSES, TOKENS], U8, align_bytes=64)
 
-        def chunk_cols(c):
-            return slice(c * CHUNK, (c + 1) * CHUNK)
+        def turn(rows_sb, first, grouped, copies):
+            words = grouped[:].bitcast(F32).rearrange("p (g r u) -> p g r u", g=PASSES, u=2)
+            offset = first % (words.shape[2] // P)
+            for k in range(len(copies)):
+                row_words = rows_sb[:, first + k, :].bitcast(F32)
+                flipped = psum.tile([P, BANK], F32, tag="bank")
+                for gu in range(flip_count):
+                    cols = slice(gu * P, (gu + 1) * P)
+                    nc.tensor.transpose(flipped[:, cols], row_words[:, cols], ident[:])
+                copies[k](
+                    out=words[:, :, (offset + k) * P : (offset + k + 1) * P, :],
+                    in_=flipped[:].rearrange("p (g u r) -> p g r u", g=PASSES, u=2),
+                )
 
-        def flip(rows_sb, r):
-            words = rows_sb[:, r, :].bitcast(F32)
-            flipped = psum.tile([P, BANK], F32, tag="bank")
-            for gu in range(PASSES * 2):
-                cols = slice(gu * P, (gu + 1) * P)
-                nc.tensor.transpose(flipped[:, cols], words[:, cols], ident[:])
-            return flipped
+        def new_pair():
+            grouped = stage.tile([P, PAIR * WIDTH], BF16, align_bytes=64, tag="pair")
+            return grouped
 
-        def regroup(flipped, grouped, r, copy):
-            grouped_words = grouped[:].bitcast(F32).rearrange("p (g r u) -> p g r u", g=PASSES, u=2)
-            copy(
-                out=grouped_words[:, :, r * P : (r + 1) * P, :],
-                in_=flipped[:].rearrange("p (g u r) -> p g r u", g=PASSES, u=2),
-            )
+        def new_half():
+            grouped = stage.tile([P, HALF * WIDTH], BF16, align_bytes=64, tag="half", bufs=2)
+            return grouped
 
-        def quantise_rows(grouped, codes, scales, first, count):
-            unit = first // 2
+        def pack_pair(grouped, codes, scales, block):
             nc.vector.quantize_mx(
-                out=codes[:, unit].rearrange("p g r -> p (g r)").bitcast(FP8X4),
-                scales=scales[:, unit].rearrange("p g r -> p (g r)"),
+                out=codes[:, block].rearrange("p g r -> p (g r)").bitcast(FP8X4),
+                scales=scales[:, block].rearrange("p g r -> p (g r)"),
                 in_=grouped[:],
             )
 
-        V = nc.vector.tensor_copy
-        S = nc.scalar.copy
+        def pack_half(grouped, codes, scales, block, g):
+            nc.vector.quantize_mx(
+                out=codes[:, block, g, :].bitcast(FP8X4),
+                scales=scales[:, block, g, :],
+                in_=grouped[:, g * HALF * P * PACK : (g + 1) * HALF * P * PACK],
+            )
 
-        def flip_rows(rows_sb, first, copies):
-            grouped = stage.tile([P, len(copies) * WIDTH], BF16, align_bytes=64, tag="grouped%d" % len(copies))
-            for r in range(len(copies)):
-                flipped = flip(rows_sb, first + r)
-                regroup(flipped, grouped, r, copies[r])
-            return grouped
+        def pack_pair_of_half(grouped, codes, scales, pair):
+            cols = slice(pair * PAIR * P, (pair + 1) * PAIR * P)
+            for g in range(PASSES):
+                nc.vector.quantize_mx(
+                    out=codes[:, 0, g, cols].bitcast(FP8X4),
+                    scales=scales[:, 0, g, cols],
+                    in_=grouped[:, g * PAIR * P * PACK : (g + 1) * PAIR * P * PACK],
+                )
 
-        b1_col = keep.tile([P, ROW_TILES], F32)
+        def w1_operand(j, g):
+            cols = slice(j % PAIR * P, (j % PAIR + 1) * P)
+            return dict(
+                lhsT=w1_codes[:, j // PAIR, g, cols].bitcast(FP8X4), lhsT_scale=w1_scales[:, j // PAIR, g, cols]
+            )
 
-        def hidden_sum(i, gf, h_sum, k):
-            tokens = slice(i % 2 * P, (i % 2 + 1) * P)
+        def x_operand(first, count, g):
+            if first < HALF:
+                cols = slice(first * P, (first + count) * P)
+                return dict(rhs=xa_codes[:, 0, g, cols].bitcast(FP8X4), rhs_scale=xa_scales[:, 0, g, cols])
+            block = (first - HALF) // PAIR
+            return dict(rhs=xb_codes[:, block, g, :].bitcast(FP8X4), rhs_scale=xb_scales[:, block, g, :])
+
+        def hidden_on_vector(i, h_sum):
             acc = psum.tile([P, PACK, P], F32, tag="bank")
             for t in range(PACK):
-                j = gf * PACK + t
-                units = slice(j % 2 * P, (j % 2 + 1) * P)
                 for g in range(PASSES):
                     nc.tensor.matmul_mx(
-                        out=acc[:, t, :],
-                        lhsT=w1_codes[:, j // 2, g, units].bitcast(FP8X4),
-                        lhsT_scale=w1_scales[:, j // 2, g, units],
-                        rhs=x_codes[:, i // 2, g, tokens].bitcast(FP8X4),
-                        rhs_scale=x_scales[:, i // 2, g, tokens],
-                        start=(g == 0),
-                        stop=(g == PASSES - 1),
+                        out=acc[:, t, :], start=(g == 0), stop=(g == PASSES - 1),
+                        **w1_operand(t, g), **x_operand(i, 1, g),
                     )
             nc.vector.tensor_tensor(
-                out=h_sum[:, k * BANK : (k + 1) * BANK].rearrange("p (n t) -> p n t", t=PACK),
+                out=h_sum[:, i * BANK : (i + 1) * BANK].rearrange("p (n t) -> p n t", t=PACK),
                 in0=acc[:].rearrange("p t n -> p n t"),
-                in1=b1_col[:, gf * PACK : (gf + 1) * PACK].unsqueeze(1).to_broadcast([P, P, PACK]),
+                in1=b1_col[:, 0:PACK].unsqueeze(1).to_broadcast([P, P, PACK]),
                 op=ALU.add,
             )
 
-        def hidden_row(first, count, rows, j):
-            units = slice(j % 2 * P, (j % 2 + 1) * P)
-            acc = psum.tile([P, BANK], F32, tag="bank")
-            for k in range(count // 2):
+        def hidden_on_scalar(first, count, gf, rows, tiles):
+            n = count * P
+            for t in tiles:
+                j = gf * PACK + t
+                acc = psum.tile([P, BANK], F32, tag="bank")
                 for g in range(PASSES):
                     nc.tensor.matmul_mx(
-                        out=acc[:, k * UNIT : (k + 1) * UNIT],
-                        lhsT=w1_codes[:, j // 2, g, units].bitcast(FP8X4),
-                        lhsT_scale=w1_scales[:, j // 2, g, units],
-                        rhs=x_codes[:, first // 2 + k, g, :].bitcast(FP8X4),
-                        rhs_scale=x_scales[:, first // 2 + k, g, :],
-                        start=(g == 0),
-                        stop=(g == PASSES - 1),
+                        out=acc[:, 0:n], start=(g == 0), stop=(g == PASSES - 1),
+                        **w1_operand(j, g), **x_operand(first, count, g),
                     )
-            nc.scalar.activation(
-                out=rows[:, j % PACK, 0 : count * P], in_=acc[:, 0 : count * P], func=FUNC.Relu,
-                bias=b1_col[:, j : j + 1], scale=1.0,
-            )
+                nc.scalar.activation(
+                    out=rows[:, t, 0:n], in_=acc[:, 0:n], func=FUNC.Relu, bias=b1_col[:, j : j + 1], scale=1.0
+                )
 
         def new_rows():
-            rows = hidden.tile([P, PACK, CHUNK], BF16, tag="rows", bufs=3)
+            rows = hidden.tile([P, PACK, HALF * P], BF16, tag="rows")
             return rows
+
+        def new_hidden():
+            h_grouped = hidden.tile([P, HALF * P * PACK], BF16, align_bytes=64, tag="h_grouped")
+            return h_grouped
 
         def interleave(rows, count, h_grouped, copies):
             width = count * P // len(copies)
-            for n in range(len(copies)):
-                copies[n](
-                    out=h_grouped[:, n * width * PACK : (n + 1) * width * PACK].rearrange(
+            for k in range(len(copies)):
+                copies[k](
+                    out=h_grouped[:, k * width * PACK : (k + 1) * width * PACK].rearrange(
                         "p (c i t) -> p c t i", i=4, t=PACK
                     ),
-                    in_=rows[:, :, n * width : (n + 1) * width].rearrange("p t (c i) -> p c t i", i=4),
+                    in_=rows[:, :, k * width : (k + 1) * width].rearrange("p t (c i) -> p c t i", i=4),
                 )
-
-        def new_hidden():
-            h_grouped = hidden.tile([P, CHUNK * PACK], BF16, align_bytes=64, tag="h_grouped", bufs=3)
-            return h_grouped
 
         def quantise_hidden(first, count, gf, h_grouped):
             tokens = slice(first * P, (first + count) * P)
@@ -215,236 +232,177 @@ def tile_transformerblock_pb_kernel(tc, x_norm1, W1, b1, W2, b2, ln_gamma, ln_be
             )
 
         xb = keep.tile([P, ROW_TILES, WIDTH], F32)
-        ident_bf = keep.tile([P, P], BF16)
 
-        def residual_plus_bias_pe(i, copy):
+        def residual_on_tensor(i):
             for n in range(WIDTH // BANK):
                 cols = slice(n * BANK, (n + 1) * BANK)
                 acc = psum.tile([P, BANK], F32, tag="bank")
                 nc.tensor.matmul(acc[:], lhsT=ident_bf[:], rhs=x_sb[:, i, cols], start=True, stop=False)
-                nc.tensor.matmul(acc[:], lhsT=ones[:], rhs=vec_rows[:, cols], start=False, stop=True)
-                copy(out=xb[:, i, cols], in_=acc[:])
+                nc.tensor.matmul(acc[:], lhsT=ones[:], rhs=b2_row[:, cols], start=False, stop=True)
+                scalar_copy(out=xb[:, i, cols], in_=acc[:])
 
-        def residual_plus_bias_v(i):
+        def residual_on_vector(i):
             nc.vector.tensor_tensor(out=xb[:, i, :], in0=x_sb[:, i, :], in1=b2_all[:], op=ALU.add)
 
-        def second_product(i, n):
+        accs, ys, y_sums, means, sq_sums, rstds, zs = {}, {}, {}, {}, {}, {}, {}
+
+        def products(i):
             tokens = slice(i * P, (i + 1) * P)
-            acc = psum.tile([P, BANK], F32, tag="bank")
-            for k in range(2):
+            for n in range(WIDTH // BANK):
+                acc = psum.tile([P, BANK], F32, tag="bank")
                 for gf in range(PASSES):
                     nc.tensor.matmul_mx(
-                        out=acc[:, k * UNIT : (k + 1) * UNIT],
+                        out=acc[:],
                         lhsT=h_codes[:, gf, tokens].bitcast(FP8X4),
                         lhsT_scale=h_scales[:, gf, tokens],
-                        rhs=w2_codes[:, 2 * n + k, gf, :].bitcast(FP8X4),
-                        rhs_scale=w2_scales[:, 2 * n + k, gf, :],
+                        rhs=w2_codes[:, n, gf, :].bitcast(FP8X4),
+                        rhs_scale=w2_scales[:, n, gf, :],
                         start=(gf == 0),
                         stop=(gf == PASSES - 1),
                     )
-            return acc
+                accs[i, n] = acc
 
-        def new_y():
+        def sums(i):
             y = norm.tile([P, WIDTH], F32, tag="y")
             y_sum = small.tile([P, WIDTH // BANK], F32, tag="y_sum")
-            return y, y_sum
+            ys[i], y_sums[i] = y, y_sum
+            for n in range(WIDTH // BANK):
+                cols = slice(n * BANK, (n + 1) * BANK)
+                nc.vector.scalar_tensor_tensor(
+                    out=y[:, cols], in0=accs[i, n][:], scalar=1.0, in1=xb[:, i, cols],
+                    op0=ALU.mult, op1=ALU.add, accum_out=y_sum[:, n : n + 1],
+                )
 
-        def residual_sum(i, n, y, y_sum, acc):
-            cols = slice(n * BANK, (n + 1) * BANK)
-            nc.vector.scalar_tensor_tensor(
-                out=y[:, cols], in0=acc[:], scalar=1.0, in1=xb[:, i, cols],
-                op0=ALU.mult, op1=ALU.add, accum_out=y_sum[:, n : n + 1],
-            )
-
-        def mean(y_sum):
+        def averaged(i):
             neg_mean = small.tile([P, 1], F32, tag="neg_mean")
             nc.vector.tensor_scalar(
-                out=neg_mean[:], in0=y_sum[:, 0:1], scalar1=y_sum[:, 1:2], scalar2=-1.0 / WIDTH,
+                out=neg_mean[:], in0=y_sums[i][:, 0:1], scalar1=y_sums[i][:, 1:2], scalar2=-1.0 / WIDTH,
                 op0=ALU.add, op1=ALU.mult,
             )
-            return neg_mean
+            means[i] = neg_mean
 
-        def square(y, neg_mean):
+        def squared(i):
             squares = norm.tile([P, WIDTH], BF16, tag="squares", bufs=1)
             sq_sum = small.tile([P, 1], F32, tag="sq_sum")
             nc.scalar.activation(
-                out=squares[:], in_=y[:], func=FUNC.Square, bias=neg_mean[:, 0:1], scale=1.0, accum_out=sq_sum[:]
+                out=squares[:], in_=ys[i][:], func=FUNC.Square, bias=means[i][:, 0:1], scale=1.0, accum_out=sq_sum[:]
             )
-            return sq_sum
+            sq_sums[i] = sq_sum
 
-        def deviation(sq_sum):
+        def deviated(i):
             rstd = small.tile([P, 1], F32, tag="rstd")
             nc.scalar.activation(
-                out=rstd[:], in_=sq_sum[:], func=FUNC.Abs_reciprocal_sqrt, bias=eps[:, 0:1], scale=1.0 / WIDTH
+                out=rstd[:], in_=sq_sums[i][:], func=FUNC.Abs_reciprocal_sqrt, bias=eps[:, 0:1], scale=1.0 / WIDTH
             )
-            return rstd
+            rstds[i] = rstd
 
-        def scale_shift(y, neg_mean):
+        def scaled(i):
             z = norm.tile([P, WIDTH], F32, tag="z", bufs=6)
             nc.vector.scalar_tensor_tensor(
-                out=z[:], in0=y[:], scalar=neg_mean[:, 0:1], in1=gamma_all[:], op0=ALU.add, op1=ALU.mult
+                out=z[:], in0=ys[i][:], scalar=means[i][:, 0:1], in1=gamma_all[:], op0=ALU.add, op1=ALU.mult
             )
-            return z
+            zs[i] = z
 
-        def finish(i, z, rstd, pieces=1):
+        def finished(i, pieces=1):
             width = WIDTH // pieces
             for n in range(pieces):
                 cols = slice(n * width, (n + 1) * width)
                 nc.vector.scalar_tensor_tensor(
-                    out=z[:, cols], in0=z[:, cols], scalar=rstd[:, 0:1], in1=beta_all[:, cols], op0=ALU.mult, op1=ALU.add
+                    out=zs[i][:, cols], in0=zs[i][:, cols], scalar=rstds[i][:, 0:1], in1=beta_all[:, cols],
+                    op0=ALU.mult, op1=ALU.add,
                 )
-                nc.sync.dma_start(out=out_view[:, i, cols], in_=z[:, cols])
+                nc.sync.dma_start(out=out_view[:, i, cols], in_=zs[i][:, cols])
 
-        ys, means, sqs, rstds, zs, accs = {}, {}, {}, {}, {}, {}
-
-        def new_sum():
-            h_sum = hidden.tile([P, CHUNK * PACK], BF16, align_bytes=64, tag="h_sum")
-            return h_sum
-
-        def relu(h_sum):
-            nc.vector.tensor_scalar_max(out=h_sum[:], in0=h_sum[:], scalar1=0.0)
-
-        def products(i):
-            accs[i] = [second_product(i, 0), second_product(i, 1)]
-
-        def sums(i, n):
-            if n == 0:
-                ys[i] = new_y()
-            residual_sum(i, n, ys[i][0], ys[i][1], accs[i][n])
-
-        def squared(i):
-            sqs[i] = square(ys[i][0], means[i])
-
-        def deviated(i):
-            rstds[i] = deviation(sqs[i])
-
-        def averaged(i):
-            means[i] = mean(ys[i][1])
-
-        def scaled(i):
-            zs[i] = scale_shift(ys[i][0], means[i])
-
-        def finished(i, pieces=1):
-            finish(i, zs[i], rstds[i], pieces)
-
-
-        PIECES = (
-            (x_sb, x_codes, x_scales, 0), (w1_sb, w1_codes, w1_scales, 0), (w1_sb, w1_codes, w1_scales, 2),
-            (x_sb, x_codes, x_scales, 2), (w1_sb, w1_codes, w1_scales, 4), (w1_sb, w1_codes, w1_scales, 6),
-            (w2_sb, w2_codes, w2_scales, 0), (w2_sb, w2_codes, w2_scales, 2), (w2_sb, w2_codes, w2_scales, 4),
-            (w2_sb, w2_codes, w2_scales, 6), (x_sb, x_codes, x_scales, 4), (x_sb, x_codes, x_scales, 6),
-        )
-        packed = {}
-
-        def turn(n, copies=(S, S)):
-            packed[n] = flip_rows(PIECES[n][0], PIECES[n][3], copies)
-
-        def pack(n):
-            quantise_rows(packed[n], PIECES[n][1], PIECES[n][2], PIECES[n][3], 2)
-
-        turn(0, (S, V))
-        turn(1, (S, V))
-        pack(0)
-        turn(2, (S, V))
-        nc.vector.tensor_copy(out=b1_col[:], in_=b1_pairs[:])
-        pack(1)
-        nc.vector.tensor_copy(out=ident_bf[:], in_=ident[:])
-        turn(3, (S, S))
-        pack(2)
-        turn(4, (S, S))
-        pack(3)
-        s0 = new_sum()
-        hidden_sum(0, 0, s0, 0)
-        hidden_sum(1, 0, s0, 1)
-        turn(5, (S, S))
-        pack(4)
-        turn(6, (S, S))
-        hidden_sum(2, 0, s0, 2)
-        pack(5)
-        hidden_sum(3, 0, s0, 3)
-        r1 = new_rows()
-        g1 = new_hidden()
-        for j in range(4, 6):
-            hidden_row(0, 4, r1, j)
-        pack(6)
-        relu(s0)
-        turn(7, (S, V))
-        for j in range(6, 8):
-            hidden_row(0, 4, r1, j)
-        quantise_hidden(0, 4, 0, s0)
-        turn(8, (S, S))
-        pack(7)
-        interleave(r1, 4, g1, (V, V))
-        turn(9, (S, S))
-        pack(8)
-        quantise_hidden(0, 4, 1, g1)
-        pack(9)
-        residual_plus_bias_pe(0, S)
-        turn(10, (S, S))
+        x0, w1a, w1b, x1, w1c = new_pair(), new_pair(), new_pair(), new_pair(), new_pair()
+        turn(x_sb, 0, x0, (scalar_copy, vector_copy))
+        turn(w1_sb, 0, w1a, (scalar_copy, scalar_copy))
+        pack_pair_of_half(x0, xa_codes, xa_scales, 0)
+        turn(w1_sb, 2, w1b, (scalar_copy, vector_copy))
+        vector_copy(out=b1_col[:], in_=b1_pairs[:])
+        pack_pair(w1a, w1_codes, w1_scales, 0)
+        turn(x_sb, 2, x1, (scalar_copy, scalar_copy))
+        pack_pair(w1b, w1_codes, w1_scales, 1)
+        turn(w1_sb, 4, w1c, (scalar_copy, scalar_copy))
+        pack_pair_of_half(x1, xa_codes, xa_scales, 1)
+        h_sum = new_hidden()
+        hidden_on_vector(0, h_sum)
+        hidden_on_vector(1, h_sum)
+        w1d = new_pair()
+        turn(w1_sb, 6, w1d, (scalar_copy, scalar_copy))
+        pack_pair(w1c, w1_codes, w1_scales, 2)
+        residual_on_vector(2)
+        w2_first = new_half()
+        turn(w2_sb, 0, w2_first, (scalar_copy, scalar_copy))
+        hidden_on_vector(2, h_sum)
+        pack_pair(w1d, w1_codes, w1_scales, 3)
+        hidden_on_vector(3, h_sum)
+        rows, h_grouped = new_rows(), new_hidden()
+        hidden_on_scalar(0, HALF, 1, rows, (0, 1))
+        nc.vector.tensor_scalar_max(out=h_sum[:], in0=h_sum[:], scalar1=0.0)
+        turn(w2_sb, 2, w2_first, (scalar_copy, scalar_copy))
+        hidden_on_scalar(0, HALF, 1, rows, (2, 3))
+        quantise_hidden(0, HALF, 0, h_sum)
+        w2_second = new_half()
+        turn(w2_sb, 4, w2_second, (scalar_copy, scalar_copy))
+        pack_half(w2_first, w2_codes, w2_scales, 0, 0)
+        pack_half(w2_first, w2_codes, w2_scales, 0, 1)
+        interleave(rows, HALF, h_grouped, (vector_copy,))
+        turn(w2_sb, 6, w2_second, (scalar_copy, scalar_copy))
+        quantise_hidden(0, HALF, 1, h_grouped)
+        pack_half(w2_second, w2_codes, w2_scales, 1, 0)
+        pack_half(w2_second, w2_codes, w2_scales, 1, 1)
+        residual_on_tensor(0)
+        x2, x3 = new_pair(), new_pair()
+        turn(x_sb, 4, x2, (scalar_copy, scalar_copy))
         products(0)
-        residual_plus_bias_pe(1, S)
+        residual_on_tensor(1)
 
-        rows, grouped = {}, {}
+        parts = {}
 
         def begin(first, gf):
-            rows[first, gf] = new_rows()
-            grouped[first, gf] = new_hidden()
+            parts[first, gf] = (new_rows(), new_hidden())
+            hidden_on_scalar(first, PAIR, gf, parts[first, gf][0], range(PACK))
 
-        def hidden_pair(first, gf):
-            begin(first, gf)
-            for j in range(4 * gf, 4 * gf + 4):
-                hidden_row(first, 2, rows[first, gf], j)
+        def lay(first, gf, copies):
+            interleave(parts[first, gf][0], PAIR, parts[first, gf][1], copies)
 
-        def work_before(i):
-            if i == 0:
-                pack(10)
-            if i == 99:
-                pack(11)
-            if i == 2:
-                quantise_hidden(4, 2, 0, grouped[4, 0])
-            if i == 3:
-                quantise_hidden(4, 2, 1, grouped[4, 1])
-            if i == 4:
-                quantise_hidden(6, 2, 0, grouped[6, 0])
-            if i == 5:
-                quantise_hidden(6, 2, 1, grouped[6, 1])
+        def quantise_part(first, gf):
+            quantise_hidden(first, PAIR, gf, parts[first, gf][1])
 
-        def work(i):
-            if i == 0:
-                hidden_pair(4, 0)
-            if i == 1:
-                interleave(rows[4, 0], 2, grouped[4, 0], (S,))
-                residual_plus_bias_v(2)
-                hidden_pair(4, 1)
-                turn(11)
-            if i == 2:
-                interleave(rows[4, 1], 2, grouped[4, 1], (S,))
-                residual_plus_bias_v(3)
-                pack(11)
-                hidden_pair(6, 0)
-            if i == 3:
-                interleave(rows[6, 0], 2, grouped[6, 0], (S,))
-                hidden_pair(6, 1)
-            if i == 4:
-                interleave(rows[6, 1], 2, grouped[6, 1], (S,))
-
-        for i in range(8):
-            sums(i, 0)
-            sums(i, 1)
+        for i in range(ROW_TILES):
+            sums(i)
             if i > 0:
                 scaled(i - 1)
             averaged(i)
-            work_before(i)
+            if i == 0:
+                pack_pair(x2, xb_codes, xb_scales, 0)
+            if 2 <= i < 6:
+                quantise_part(4 + (i - 2) // 2 * 2, i % 2)
             squared(i)
             if i in (2, 3):
-                residual_plus_bias_pe(i + 2, S)
-            if i < 7:
+                residual_on_tensor(i + 2)
+            if i + 1 < ROW_TILES:
                 products(i + 1)
             if i > 1:
                 finished(i - 2)
-            work(i)
+            if i == 0:
+                begin(4, 0)
+            if i == 1:
+                lay(4, 0, (scalar_copy,))
+                begin(4, 1)
+                turn(x_sb, 6, x3, (scalar_copy, scalar_copy))
+            if i == 2:
+                lay(4, 1, (scalar_copy,))
+                residual_on_vector(3)
+                pack_pair(x3, xb_codes, xb_scales, 1)
+                begin(6, 0)
+            if i == 3:
+                lay(6, 0, (scalar_copy,))
+                begin(6, 1)
+            if i == 4:
+                lay(6, 1, (scalar_copy,))
             if i in (4, 5):
-                residual_plus_bias_pe(i + 2, S)
+                residual_on_tensor(i + 2)
             deviated(i)
         finished(6)
         scaled(7)

@@ -72,7 +72,6 @@ def tile_transformerblock_pb_kernel(tc, x_norm1, W1, b1, W2, b2, ln_gamma, ln_be
         load_x(2, 4)
         load_w1(4, 6)
         load_w1(6, 8)
-        nc.sync.dma_start(out=b2_all[:], in_=b2.partition_broadcast(P))
         load_w2(0, 2)
         load_w2(2, 4)
         load_w2(4, 6)
@@ -233,16 +232,16 @@ def tile_transformerblock_pb_kernel(tc, x_norm1, W1, b1, W2, b2, ln_gamma, ln_be
 
         xb = keep.tile([P, ROW_TILES, WIDTH], F32)
 
-        def residual_on_tensor(i):
-            for n in range(WIDTH // BANK):
+        def residual_on_tensor(i, halves=(0, 1)):
+            for n in halves:
                 cols = slice(n * BANK, (n + 1) * BANK)
                 acc = psum.tile([P, BANK], F32, tag="bank")
                 nc.tensor.matmul(acc[:], lhsT=ident_bf[:], rhs=x_sb[:, i, cols], start=True, stop=False)
                 nc.tensor.matmul(acc[:], lhsT=ones[:], rhs=b2_row[:, cols], start=False, stop=True)
                 scalar_copy(out=xb[:, i, cols], in_=acc[:])
 
-        def residual_on_vector(i):
-            nc.vector.tensor_tensor(out=xb[:, i, :], in0=x_sb[:, i, :], in1=b2_all[:], op=ALU.add)
+        def residual_on_vector(i, cols=slice(0, WIDTH)):
+            nc.vector.tensor_tensor(out=xb[:, i, cols], in0=x_sb[:, i, cols], in1=b2_all[:, cols], op=ALU.add)
 
         accs, ys, y_sums, means, sq_sums, rstds, zs = {}, {}, {}, {}, {}, {}, {}
 
@@ -278,6 +277,14 @@ def tile_transformerblock_pb_kernel(tc, x_norm1, W1, b1, W2, b2, ln_gamma, ln_be
             nc.vector.tensor_scalar(
                 out=neg_mean[:], in0=y_sums[i][:, 0:1], scalar1=y_sums[i][:, 1:2], scalar2=-1.0 / WIDTH,
                 op0=ALU.add, op1=ALU.mult,
+            )
+            means[i] = neg_mean
+
+        def averaged_on_scalar(i):
+            neg_mean = small.tile([P, 1], F32, tag="neg_mean")
+            halves = small.tile([P, WIDTH // BANK], F32, tag="halves")
+            nc.scalar.activation(
+                out=halves[:], in_=y_sums[i][:], func=FUNC.Copy, scale=-1.0 / WIDTH, accum_out=neg_mean[:]
             )
             means[i] = neg_mean
 
@@ -317,6 +324,11 @@ def tile_transformerblock_pb_kernel(tc, x_norm1, W1, b1, W2, b2, ln_gamma, ln_be
         turn(x_sb, 0, x0, (scalar_copy, vector_copy))
         turn(w1_sb, 0, w1a, (scalar_copy, scalar_copy))
         pack_pair_of_half(x0, xa_codes, xa_scales, 0)
+        b2_bank = psum.tile([P, WIDTH], BF16, tag="bank")
+        for n in range(WIDTH // BANK):
+            cols = slice(n * BANK, (n + 1) * BANK)
+            nc.tensor.matmul(b2_bank[:, cols], lhsT=ones[:], rhs=b2_row[:, cols], start=True, stop=True)
+        scalar_copy(out=b2_all[:], in_=b2_bank[:])
         turn(w1_sb, 2, w1b, (scalar_copy, vector_copy))
         vector_copy(out=b1_col[:], in_=b1_pairs[:])
         pack_pair(w1a, w1_codes, w1_scales, 0)
@@ -373,7 +385,10 @@ def tile_transformerblock_pb_kernel(tc, x_norm1, W1, b1, W2, b2, ln_gamma, ln_be
             sums(i)
             if i > 0:
                 scaled(i - 1)
-            averaged(i)
+            if i > 4:
+                averaged_on_scalar(i)
+            else:
+                averaged(i)
             if i == 0:
                 pack_pair(x2, xb_codes, xb_scales, 0)
             if 2 <= i < 6:
@@ -401,8 +416,11 @@ def tile_transformerblock_pb_kernel(tc, x_norm1, W1, b1, W2, b2, ln_gamma, ln_be
                 begin(6, 1)
             if i == 4:
                 lay(6, 1, (scalar_copy,))
-            if i in (4, 5):
-                residual_on_tensor(i + 2)
+            if i == 4:
+                residual_on_tensor(6)
+            if i == 5:
+                residual_on_tensor(7, (0,))
+                residual_on_vector(7, slice(BANK, WIDTH))
             deviated(i)
         finished(6)
         scaled(7)

@@ -25,6 +25,7 @@ HALF = 4
 PAIR = 2
 LN_EPS = 1e-5
 
+SUMMED_BY_SCALAR = (5, 6, 7)
 FLOPS = 2 * 2 * TOKENS * WIDTH * WIDTH
 
 
@@ -80,15 +81,13 @@ def tile_transformerblock_pb_kernel(tc, x_norm1, W1, b1, W2, b2, ln_gamma, ln_be
         nc.sync.dma_start(out=gamma_all[:], in_=ln_gamma.partition_broadcast(P))
         nc.sync.dma_start(out=beta_all[:], in_=ln_beta.partition_broadcast(P))
 
-        b2_row = keep.tile([P, WIDTH], BF16)
-        nc.vector.memset(b2_row[:].bitcast(I32), 0)
-        b1_pairs = keep.tile([P, ROW_TILES], BF16)
-        with nc.allow_non_contiguous_dma(reason="b1 is 2 KiB, loaded once as 4-byte pairs"):
+        rows_12 = keep.tile([P, 2 * WIDTH], BF16)
+        for v, vec in enumerate((b1, b2)):
             nc.scalar.dma_start(
-                out=b1_pairs[:].rearrange("p (a e) -> p a e", e=2),
-                in_=b1.rearrange("(a p e) -> p a e", p=P, e=2),
+                out=rows_12[P - 1 : P, v * WIDTH : (v + 1) * WIDTH], in_=vec.rearrange("(o d) -> o d", o=1)
             )
-        nc.scalar.dma_start(out=b2_row[0:1, :], in_=b2.rearrange("(o d) -> o d", o=1))
+        nc.vector.memset(rows_12[0 : P - 1, :].bitcast(I32), 0)
+        b1_row, b2_row = rows_12[:, 0:WIDTH], rows_12[:, WIDTH : 2 * WIDTH]
         ident = keep.tile([P, P], F32)
         make_identity(nc, ident[:])
         ident_bf = keep.tile([P, P], BF16)
@@ -268,8 +267,8 @@ def tile_transformerblock_pb_kernel(tc, x_norm1, W1, b1, W2, b2, ln_gamma, ln_be
             for n in range(WIDTH // BANK):
                 cols = slice(n * BANK, (n + 1) * BANK)
                 nc.vector.scalar_tensor_tensor(
-                    out=y[:, cols], in0=accs[i, n][:], scalar=1.0, in1=xb[:, i, cols],
-                    op0=ALU.mult, op1=ALU.add, accum_out=y_sum[:, n : n + 1],
+                    out=y[:, cols], in0=accs[i, n][:], scalar=1.0, in1=xb[:, i, cols], op0=ALU.mult, op1=ALU.add,
+                    **({} if i in SUMMED_BY_SCALAR else dict(accum_out=y_sum[:, n : n + 1])),
                 )
 
         def averaged(i):
@@ -282,10 +281,8 @@ def tile_transformerblock_pb_kernel(tc, x_norm1, W1, b1, W2, b2, ln_gamma, ln_be
 
         def averaged_on_scalar(i):
             neg_mean = small.tile([P, 1], F32, tag="neg_mean")
-            halves = small.tile([P, WIDTH // BANK], F32, tag="halves")
-            nc.scalar.activation(
-                out=halves[:], in_=y_sums[i][:], func=FUNC.Copy, scale=-1.0 / WIDTH, accum_out=neg_mean[:]
-            )
+            copied = norm.tile([P, WIDTH], BF16, tag="squares", bufs=1)
+            nc.scalar.activation(out=copied[:], in_=ys[i][:], func=FUNC.Copy, scale=-1.0 / WIDTH, accum_out=neg_mean[:])
             means[i] = neg_mean
 
         def squared(i):
@@ -322,16 +319,23 @@ def tile_transformerblock_pb_kernel(tc, x_norm1, W1, b1, W2, b2, ln_gamma, ln_be
 
         x0, w1a, w1b, x1, w1c = new_pair(), new_pair(), new_pair(), new_pair(), new_pair()
         turn(x_sb, 0, x0, (scalar_copy, vector_copy))
+        b1_bank = psum.tile([P, ROW_TILES], F32, tag="bank")
+        for j in range(ROW_TILES):
+            a, e = j // 2, j % 2
+            nc.tensor.matmul(
+                b1_bank[:, j : j + 1], lhsT=b1_row[:, 2 * P * a + e : 2 * P * (a + 1) : 2], rhs=ones[:, 0:1],
+                start=True, stop=True,
+            )
+        scalar_copy(out=b1_col[:], in_=b1_bank[:])
         turn(w1_sb, 0, w1a, (scalar_copy, scalar_copy))
         pack_pair_of_half(x0, xa_codes, xa_scales, 0)
+        turn(w1_sb, 2, w1b, (scalar_copy, vector_copy))
+        pack_pair(w1a, w1_codes, w1_scales, 0)
         b2_bank = psum.tile([P, WIDTH], BF16, tag="bank")
         for n in range(WIDTH // BANK):
             cols = slice(n * BANK, (n + 1) * BANK)
             nc.tensor.matmul(b2_bank[:, cols], lhsT=ones[:], rhs=b2_row[:, cols], start=True, stop=True)
         scalar_copy(out=b2_all[:], in_=b2_bank[:])
-        turn(w1_sb, 2, w1b, (scalar_copy, vector_copy))
-        vector_copy(out=b1_col[:], in_=b1_pairs[:])
-        pack_pair(w1a, w1_codes, w1_scales, 0)
         turn(x_sb, 2, x1, (scalar_copy, scalar_copy))
         pack_pair(w1b, w1_codes, w1_scales, 1)
         turn(w1_sb, 4, w1c, (scalar_copy, scalar_copy))
@@ -359,6 +363,7 @@ def tile_transformerblock_pb_kernel(tc, x_norm1, W1, b1, W2, b2, ln_gamma, ln_be
         pack_half(w2_first, w2_codes, w2_scales, 0, 0)
         pack_half(w2_first, w2_codes, w2_scales, 0, 1)
         interleave(rows, HALF, h_grouped, (vector_copy,))
+        residual_on_vector(7, slice(BANK, WIDTH))
         turn(w2_sb, 6, w2_second, (scalar_copy, scalar_copy))
         quantise_hidden(0, HALF, 1, h_grouped)
         pack_half(w2_second, w2_codes, w2_scales, 1, 0)
@@ -385,7 +390,7 @@ def tile_transformerblock_pb_kernel(tc, x_norm1, W1, b1, W2, b2, ln_gamma, ln_be
             sums(i)
             if i > 0:
                 scaled(i - 1)
-            if i > 4:
+            if i in SUMMED_BY_SCALAR:
                 averaged_on_scalar(i)
             else:
                 averaged(i)
@@ -420,7 +425,6 @@ def tile_transformerblock_pb_kernel(tc, x_norm1, W1, b1, W2, b2, ln_gamma, ln_be
                 residual_on_tensor(6)
             if i == 5:
                 residual_on_tensor(7, (0,))
-                residual_on_vector(7, slice(BANK, WIDTH))
             deviated(i)
         finished(6)
         scaled(7)

@@ -319,6 +319,16 @@ def tile_transformerblock_pb_kernel(tc, x_norm1, W1, b1, W2, b2, ln_gamma, ln_be
 
         x0, w1a, w1b, x1, w1c = new_pair(), new_pair(), new_pair(), new_pair(), new_pair()
         turn(x_sb, 0, x0, (scalar_copy, vector_copy))
+        b2_bank = psum.tile([P, WIDTH], BF16, tag="bank")
+        for n in range(WIDTH // BANK):
+            cols = slice(n * BANK, (n + 1) * BANK)
+            nc.tensor.matmul(b2_bank[:, cols], lhsT=ones[:], rhs=b2_row[:, cols], start=True, stop=True)
+        scalar_copy(out=b2_all[:], in_=b2_bank[:])
+        turn(w1_sb, 0, w1a, (scalar_copy, scalar_copy))
+        pack_pair_of_half(x0, xa_codes, xa_scales, 0)
+        residual_on_vector(0)
+        turn(w1_sb, 2, w1b, (scalar_copy, scalar_copy))
+        pack_pair(w1a, w1_codes, w1_scales, 0)
         b1_bank = psum.tile([P, ROW_TILES], F32, tag="bank")
         for j in range(ROW_TILES):
             a, e = j // 2, j % 2
@@ -327,17 +337,9 @@ def tile_transformerblock_pb_kernel(tc, x_norm1, W1, b1, W2, b2, ln_gamma, ln_be
                 start=True, stop=True,
             )
         scalar_copy(out=b1_col[:], in_=b1_bank[:])
-        turn(w1_sb, 0, w1a, (scalar_copy, scalar_copy))
-        pack_pair_of_half(x0, xa_codes, xa_scales, 0)
-        turn(w1_sb, 2, w1b, (scalar_copy, vector_copy))
-        pack_pair(w1a, w1_codes, w1_scales, 0)
-        b2_bank = psum.tile([P, WIDTH], BF16, tag="bank")
-        for n in range(WIDTH // BANK):
-            cols = slice(n * BANK, (n + 1) * BANK)
-            nc.tensor.matmul(b2_bank[:, cols], lhsT=ones[:], rhs=b2_row[:, cols], start=True, stop=True)
-        scalar_copy(out=b2_all[:], in_=b2_bank[:])
         turn(x_sb, 2, x1, (scalar_copy, scalar_copy))
         pack_pair(w1b, w1_codes, w1_scales, 1)
+        residual_on_vector(1)
         turn(w1_sb, 4, w1c, (scalar_copy, scalar_copy))
         pack_pair_of_half(x1, xa_codes, xa_scales, 1)
         h_sum = new_hidden()
@@ -346,7 +348,6 @@ def tile_transformerblock_pb_kernel(tc, x_norm1, W1, b1, W2, b2, ln_gamma, ln_be
         w1d = new_pair()
         turn(w1_sb, 6, w1d, (scalar_copy, scalar_copy))
         pack_pair(w1c, w1_codes, w1_scales, 2)
-        residual_on_vector(2)
         w2_first = new_half()
         turn(w2_sb, 0, w2_first, (scalar_copy, scalar_copy))
         hidden_on_vector(2, h_sum)
@@ -363,16 +364,16 @@ def tile_transformerblock_pb_kernel(tc, x_norm1, W1, b1, W2, b2, ln_gamma, ln_be
         pack_half(w2_first, w2_codes, w2_scales, 0, 0)
         pack_half(w2_first, w2_codes, w2_scales, 0, 1)
         interleave(rows, HALF, h_grouped, (vector_copy,))
-        residual_on_vector(7, slice(BANK, WIDTH))
         turn(w2_sb, 6, w2_second, (scalar_copy, scalar_copy))
         quantise_hidden(0, HALF, 1, h_grouped)
         pack_half(w2_second, w2_codes, w2_scales, 1, 0)
         pack_half(w2_second, w2_codes, w2_scales, 1, 1)
-        residual_on_tensor(0)
+        residual_on_vector(7, slice(BANK, WIDTH))
+        residual_on_tensor(2)
         x2, x3 = new_pair(), new_pair()
         turn(x_sb, 4, x2, (scalar_copy, scalar_copy))
         products(0)
-        residual_on_tensor(1)
+        residual_on_tensor(3)
 
         parts = {}
 
@@ -390,12 +391,12 @@ def tile_transformerblock_pb_kernel(tc, x_norm1, W1, b1, W2, b2, ln_gamma, ln_be
             sums(i)
             if i > 0:
                 scaled(i - 1)
+            if i == 0:
+                pack_pair(x2, xb_codes, xb_scales, 0)
             if i in SUMMED_BY_SCALAR:
                 averaged_on_scalar(i)
             else:
                 averaged(i)
-            if i == 0:
-                pack_pair(x2, xb_codes, xb_scales, 0)
             if 2 <= i < 6:
                 quantise_part(4 + (i - 2) // 2 * 2, i % 2)
             squared(i)
@@ -408,12 +409,11 @@ def tile_transformerblock_pb_kernel(tc, x_norm1, W1, b1, W2, b2, ln_gamma, ln_be
             if i == 0:
                 begin(4, 0)
             if i == 1:
-                lay(4, 0, (scalar_copy,))
+                lay(4, 0, (vector_copy,))
                 begin(4, 1)
                 turn(x_sb, 6, x3, (scalar_copy, scalar_copy))
             if i == 2:
                 lay(4, 1, (scalar_copy,))
-                residual_on_vector(3)
                 pack_pair(x3, xb_codes, xb_scales, 1)
                 begin(6, 0)
             if i == 3:

from contextlib import ExitStack

import concourse.mybir as mybir
from concourse.masks import make_identity

F32 = mybir.dt.float32
BF16 = mybir.dt.bfloat16
I32 = mybir.dt.int32
U32 = mybir.dt.uint32
U8 = mybir.dt.uint8
FP8X4 = mybir.dt.float8_e4m3fn_x4
FUNC = mybir.ActivationFunctionType
ALU = mybir.AluOpType

P = 128
PACK = 4
K_PASS = P * PACK
BANK = 512

TOKENS = 1024
WIDTH = 1024
PASSES = WIDTH // K_PASS
ROW_TILES = 8
HALF = 4
PAIR = 2
LN_EPS = 1e-5

SUMMED_BY_SCALAR = (5, 6, 7)
FLOPS = 2 * 2 * TOKENS * WIDTH * WIDTH


def tile_transformerblock_pb_kernel(tc, x_norm1, W1, b1, W2, b2, ln_gamma, ln_beta, out):
    nc = tc.nc
    x_view = x_norm1.flatten_outer_dims().rearrange("(p i) d -> p i d", i=ROW_TILES)
    out_view = out.flatten_outer_dims().rearrange("(p i) d -> p i d", i=ROW_TILES)
    w1_view = W1.rearrange("(a p e) k -> p a (e k)", p=P, e=2)
    w2_view = W2.rearrange("(j p) f -> p j f", p=P)

    with ExitStack() as ctx:
        keep = ctx.enter_context(tc.tile_pool(name="keep", bufs=1))
        stage = ctx.enter_context(tc.tile_pool(name="stage", bufs=3))
        hidden = ctx.enter_context(tc.tile_pool(name="hidden", bufs=3))
        norm = ctx.enter_context(tc.tile_pool(name="norm", bufs=4))
        small = ctx.enter_context(tc.tile_pool(name="small", bufs=4))
        psum = ctx.enter_context(tc.psum_pool(name="psum", bufs=8))
        ctx.enter_context(tc.manual_schedule())

        vector_copy = nc.vector.tensor_copy
        scalar_copy = nc.scalar.copy

        x_sb = keep.tile([P, ROW_TILES, WIDTH], BF16)
        w1_sb = keep.tile([P, ROW_TILES, WIDTH], BF16)
        w2_sb = keep.tile([P, ROW_TILES, WIDTH], BF16)
        b2_all = keep.tile([P, WIDTH], BF16)
        gamma_all = keep.tile([P, WIDTH], BF16)
        beta_all = keep.tile([P, WIDTH], BF16)

        def load_x(first, last):
            nc.sync.dma_start(out=x_sb[:, first:last, :], in_=x_view[:, first:last, :])

        def load_w1(first, last):
            nc.sync.dma_start(
                out=w1_sb[:, first:last, :].rearrange("p (a e) k -> p a (e k)", e=2),
                in_=w1_view[:, first // 2 : last // 2, :],
            )

        def load_w2(first, last):
            nc.sync.dma_start(out=w2_sb[:, first:last, :], in_=w2_view[:, first:last, :])

        load_x(0, 2)
        load_w1(0, 2)
        load_w1(2, 4)
        load_x(2, 4)
        load_w1(4, 6)
        load_w1(6, 8)
        load_w2(0, 2)
        load_w2(2, 4)
        load_w2(4, 6)
        load_w2(6, 8)
        load_x(4, 8)
        nc.sync.dma_start(out=gamma_all[:], in_=ln_gamma.partition_broadcast(P))
        nc.sync.dma_start(out=beta_all[:], in_=ln_beta.partition_broadcast(P))

        rows_12 = keep.tile([P, 2 * WIDTH], BF16)
        for v, vec in enumerate((b1, b2)):
            nc.scalar.dma_start(
                out=rows_12[P - 1 : P, v * WIDTH : (v + 1) * WIDTH], in_=vec.rearrange("(o d) -> o d", o=1)
            )
        nc.vector.memset(rows_12[0 : P - 1, :].bitcast(I32), 0)
        b1_row, b2_row = rows_12[:, 0:WIDTH], rows_12[:, WIDTH : 2 * WIDTH]
        ident = keep.tile([P, P], F32)
        make_identity(nc, ident[:])
        ident_bf = keep.tile([P, P], BF16)
        vector_copy(out=ident_bf[:], in_=ident[:])
        ones = keep.tile([P, P], BF16)
        nc.vector.memset(ones[:], 1.0)
        eps = keep.tile([P, 1], F32)
        nc.vector.memset(eps[:], LN_EPS)
        table_first = keep.tile([P, 1], F32)
        nc.scalar.activation(out=table_first[:], in_=eps[:], func=FUNC.Abs_reciprocal_sqrt)
        b1_col = keep.tile([P, ROW_TILES], F32)

        flip_count = WIDTH // 2 // P

        def codes_and_scales(blocks, rows):
            codes = keep.tile([P, blocks, PASSES, rows], U32, align_bytes=64, name="codes_%d" % len(all_codes))
            scales = keep.tile([P, blocks, PASSES, rows], U8, align_bytes=64, name="scales_%d" % len(all_codes))
            all_codes.append(codes)
            return codes, scales

        all_codes = []
        xa_codes, xa_scales = codes_and_scales(1, HALF * P)
        xb_codes, xb_scales = codes_and_scales(2, PAIR * P)
        w1_codes, w1_scales = codes_and_scales(4, PAIR * P)
        w2_codes, w2_scales = codes_and_scales(2, HALF * P)
        h_codes = keep.tile([P, PASSES, TOKENS], U32, align_bytes=64)
        h_scales = keep.tile([P, PASSES, TOKENS], U8, align_bytes=64)

        def turn(rows_sb, first, grouped, copies):
            words = grouped[:].bitcast(F32).rearrange("p (g r u) -> p g r u", g=PASSES, u=2)
            offset = first % (words.shape[2] // P)
            for k in range(len(copies)):
                row_words = rows_sb[:, first + k, :].bitcast(F32)
                flipped = psum.tile([P, BANK], F32, tag="bank")
                for gu in range(flip_count):
                    cols = slice(gu * P, (gu + 1) * P)
                    nc.tensor.transpose(flipped[:, cols], row_words[:, cols], ident[:])
                copies[k](
                    out=words[:, :, (offset + k) * P : (offset + k + 1) * P, :],
                    in_=flipped[:].rearrange("p (g u r) -> p g r u", g=PASSES, u=2),
                )

        def new_pair():
            grouped = stage.tile([P, PAIR * WIDTH], BF16, align_bytes=64, tag="pair")
            return grouped

        def new_half():
            grouped = stage.tile([P, HALF * WIDTH], BF16, align_bytes=64, tag="half", bufs=2)
            return grouped

        def pack_pair(grouped, codes, scales, block):
            nc.vector.quantize_mx(
                out=codes[:, block].rearrange("p g r -> p (g r)").bitcast(FP8X4),
                scales=scales[:, block].rearrange("p g r -> p (g r)"),
                in_=grouped[:],
            )

        def pack_half(grouped, codes, scales, block, g):
            nc.vector.quantize_mx(
                out=codes[:, block, g, :].bitcast(FP8X4),
                scales=scales[:, block, g, :],
                in_=grouped[:, g * HALF * P * PACK : (g + 1) * HALF * P * PACK],
            )

        def pack_pair_of_half(grouped, codes, scales, pair):
            cols = slice(pair * PAIR * P, (pair + 1) * PAIR * P)
            for g in range(PASSES):
                nc.vector.quantize_mx(
                    out=codes[:, 0, g, cols].bitcast(FP8X4),
                    scales=scales[:, 0, g, cols],
                    in_=grouped[:, g * PAIR * P * PACK : (g + 1) * PAIR * P * PACK],
                )

        def w1_operand(j, g):
            cols = slice(j % PAIR * P, (j % PAIR + 1) * P)
            return dict(
                lhsT=w1_codes[:, j // PAIR, g, cols].bitcast(FP8X4), lhsT_scale=w1_scales[:, j // PAIR, g, cols]
            )

        def x_operand(first, count, g):
            if first < HALF:
                cols = slice(first * P, (first + count) * P)
                return dict(rhs=xa_codes[:, 0, g, cols].bitcast(FP8X4), rhs_scale=xa_scales[:, 0, g, cols])
            block = (first - HALF) // PAIR
            return dict(rhs=xb_codes[:, block, g, :].bitcast(FP8X4), rhs_scale=xb_scales[:, block, g, :])

        def hidden_on_vector(i, h_sum):
            acc = psum.tile([P, PACK, P], F32, tag="bank")
            for t in range(PACK):
                for g in range(PASSES):
                    nc.tensor.matmul_mx(
                        out=acc[:, t, :], start=(g == 0), stop=(g == PASSES - 1),
                        **w1_operand(t, g), **x_operand(i, 1, g),
                    )
            nc.vector.tensor_tensor(
                out=h_sum[:, i * BANK : (i + 1) * BANK].rearrange("p (n t) -> p n t", t=PACK),
                in0=acc[:].rearrange("p t n -> p n t"),
                in1=b1_col[:, 0:PACK].unsqueeze(1).to_broadcast([P, P, PACK]),
                op=ALU.add,
            )

        def hidden_on_scalar(first, count, gf, rows, tiles):
            n = count * P
            for t in tiles:
                j = gf * PACK + t
                acc = psum.tile([P, BANK], F32, tag="bank")
                for g in range(PASSES):
                    nc.tensor.matmul_mx(
                        out=acc[:, 0:n], start=(g == 0), stop=(g == PASSES - 1),
                        **w1_operand(j, g), **x_operand(first, count, g),
                    )
                nc.scalar.activation(
                    out=rows[:, t, 0:n], in_=acc[:, 0:n], func=FUNC.Relu, bias=b1_col[:, j : j + 1], scale=1.0
                )

        def new_rows():
            rows = hidden.tile([P, PACK, HALF * P], BF16, tag="rows")
            return rows

        def new_hidden():
            h_grouped = hidden.tile([P, HALF * P * PACK], BF16, align_bytes=64, tag="h_grouped")
            return h_grouped

        def interleave(rows, count, h_grouped, copies):
            width = count * P // len(copies)
            for k in range(len(copies)):
                copies[k](
                    out=h_grouped[:, k * width * PACK : (k + 1) * width * PACK].rearrange(
                        "p (c i t) -> p c t i", i=4, t=PACK
                    ),
                    in_=rows[:, :, k * width : (k + 1) * width].rearrange("p t (c i) -> p c t i", i=4),
                )

        def quantise_hidden(first, count, gf, h_grouped):
            tokens = slice(first * P, (first + count) * P)
            nc.vector.quantize_mx(
                out=h_codes[:, gf, tokens].bitcast(FP8X4),
                scales=h_scales[:, gf, tokens],
                in_=h_grouped[:, 0 : count * P * PACK],
            )

        xb = keep.tile([P, ROW_TILES, WIDTH], F32)

        def residual_on_tensor(i, halves=(0, 1)):
            for n in halves:
                cols = slice(n * BANK, (n + 1) * BANK)
                acc = psum.tile([P, BANK], F32, tag="bank")
                nc.tensor.matmul(acc[:], lhsT=ident_bf[:], rhs=x_sb[:, i, cols], start=True, stop=False)
                nc.tensor.matmul(acc[:], lhsT=ones[:], rhs=b2_row[:, cols], start=False, stop=True)
                scalar_copy(out=xb[:, i, cols], in_=acc[:])

        def residual_on_vector(i, cols=slice(0, WIDTH)):
            nc.vector.tensor_tensor(out=xb[:, i, cols], in0=x_sb[:, i, cols], in1=b2_all[:, cols], op=ALU.add)

        accs, ys, y_sums, means, sq_sums, rstds, zs = {}, {}, {}, {}, {}, {}, {}

        def products(i):
            tokens = slice(i * P, (i + 1) * P)
            for n in range(WIDTH // BANK):
                acc = psum.tile([P, BANK], F32, tag="bank")
                for gf in range(PASSES):
                    nc.tensor.matmul_mx(
                        out=acc[:],
                        lhsT=h_codes[:, gf, tokens].bitcast(FP8X4),
                        lhsT_scale=h_scales[:, gf, tokens],
                        rhs=w2_codes[:, n, gf, :].bitcast(FP8X4),
                        rhs_scale=w2_scales[:, n, gf, :],
                        start=(gf == 0),
                        stop=(gf == PASSES - 1),
                    )
                accs[i, n] = acc

        def sums(i):
            y = norm.tile([P, WIDTH], F32, tag="y")
            y_sum = small.tile([P, WIDTH // BANK], F32, tag="y_sum")
            ys[i], y_sums[i] = y, y_sum
            for n in range(WIDTH // BANK):
                cols = slice(n * BANK, (n + 1) * BANK)
                nc.vector.scalar_tensor_tensor(
                    out=y[:, cols], in0=accs[i, n][:], scalar=1.0, in1=xb[:, i, cols], op0=ALU.mult, op1=ALU.add,
                    **({} if i in SUMMED_BY_SCALAR else dict(accum_out=y_sum[:, n : n + 1])),
                )

        def averaged(i):
            neg_mean = small.tile([P, 1], F32, tag="neg_mean")
            nc.vector.tensor_scalar(
                out=neg_mean[:], in0=y_sums[i][:, 0:1], scalar1=y_sums[i][:, 1:2], scalar2=-1.0 / WIDTH,
                op0=ALU.add, op1=ALU.mult,
            )
            means[i] = neg_mean

        def averaged_on_scalar(i):
            neg_mean = small.tile([P, 1], F32, tag="neg_mean")
            copied = norm.tile([P, WIDTH], BF16, tag="squares", bufs=1)
            nc.scalar.activation(out=copied[:], in_=ys[i][:], func=FUNC.Copy, scale=-1.0 / WIDTH, accum_out=neg_mean[:])
            means[i] = neg_mean

        def squared(i):
            squares = norm.tile([P, WIDTH], BF16, tag="squares", bufs=1)
            sq_sum = small.tile([P, 1], F32, tag="sq_sum")
            nc.scalar.activation(
                out=squares[:], in_=ys[i][:], func=FUNC.Square, bias=means[i][:, 0:1], scale=1.0, accum_out=sq_sum[:]
            )
            sq_sums[i] = sq_sum

        def deviated(i):
            rstd = small.tile([P, 1], F32, tag="rstd")
            nc.scalar.activation(
                out=rstd[:], in_=sq_sums[i][:], func=FUNC.Abs_reciprocal_sqrt, bias=eps[:, 0:1], scale=1.0 / WIDTH
            )
            rstds[i] = rstd

        def scaled(i):
            z = norm.tile([P, WIDTH], F32, tag="z", bufs=6)
            nc.vector.scalar_tensor_tensor(
                out=z[:], in0=ys[i][:], scalar=means[i][:, 0:1], in1=gamma_all[:], op0=ALU.add, op1=ALU.mult
            )
            zs[i] = z

        def finished(i, pieces=1):
            width = WIDTH // pieces
            for n in range(pieces):
                cols = slice(n * width, (n + 1) * width)
                nc.vector.scalar_tensor_tensor(
                    out=zs[i][:, cols], in0=zs[i][:, cols], scalar=rstds[i][:, 0:1], in1=beta_all[:, cols],
                    op0=ALU.mult, op1=ALU.add,
                )
                nc.sync.dma_start(out=out_view[:, i, cols], in_=zs[i][:, cols])

        x0, w1a, w1b, x1, w1c = new_pair(), new_pair(), new_pair(), new_pair(), new_pair()
        turn(x_sb, 0, x0, (scalar_copy, vector_copy))
        b2_bank = psum.tile([P, WIDTH], BF16, tag="bank")
        for n in range(WIDTH // BANK):
            cols = slice(n * BANK, (n + 1) * BANK)
            nc.tensor.matmul(b2_bank[:, cols], lhsT=ones[:], rhs=b2_row[:, cols], start=True, stop=True)
        scalar_copy(out=b2_all[:], in_=b2_bank[:])
        turn(w1_sb, 0, w1a, (scalar_copy, scalar_copy))
        pack_pair_of_half(x0, xa_codes, xa_scales, 0)
        residual_on_vector(0)
        turn(w1_sb, 2, w1b, (scalar_copy, scalar_copy))
        pack_pair(w1a, w1_codes, w1_scales, 0)
        b1_bank = psum.tile([P, ROW_TILES], F32, tag="bank")
        for j in range(ROW_TILES):
            a, e = j // 2, j % 2
            nc.tensor.matmul(
                b1_bank[:, j : j + 1], lhsT=b1_row[:, 2 * P * a + e : 2 * P * (a + 1) : 2], rhs=ones[:, 0:1],
                start=True, stop=True,
            )
        scalar_copy(out=b1_col[:], in_=b1_bank[:])
        turn(x_sb, 2, x1, (scalar_copy, scalar_copy))
        pack_pair(w1b, w1_codes, w1_scales, 1)
        residual_on_vector(1)
        turn(w1_sb, 4, w1c, (scalar_copy, scalar_copy))
        pack_pair_of_half(x1, xa_codes, xa_scales, 1)
        h_sum = new_hidden()
        hidden_on_vector(0, h_sum)
        hidden_on_vector(1, h_sum)
        w1d = new_pair()
        turn(w1_sb, 6, w1d, (scalar_copy, scalar_copy))
        pack_pair(w1c, w1_codes, w1_scales, 2)
        w2_first = new_half()
        turn(w2_sb, 0, w2_first, (scalar_copy, scalar_copy))
        hidden_on_vector(2, h_sum)
        pack_pair(w1d, w1_codes, w1_scales, 3)
        hidden_on_vector(3, h_sum)
        rows, h_grouped = new_rows(), new_hidden()
        hidden_on_scalar(0, HALF, 1, rows, (0, 1))
        nc.vector.tensor_scalar_max(out=h_sum[:], in0=h_sum[:], scalar1=0.0)
        turn(w2_sb, 2, w2_first, (scalar_copy, scalar_copy))
        hidden_on_scalar(0, HALF, 1, rows, (2, 3))
        quantise_hidden(0, HALF, 0, h_sum)
        w2_second = new_half()
        turn(w2_sb, 4, w2_second, (scalar_copy, scalar_copy))
        pack_half(w2_first, w2_codes, w2_scales, 0, 0)
        pack_half(w2_first, w2_codes, w2_scales, 0, 1)
        interleave(rows, HALF, h_grouped, (vector_copy,))
        turn(w2_sb, 6, w2_second, (scalar_copy, scalar_copy))
        quantise_hidden(0, HALF, 1, h_grouped)
        pack_half(w2_second, w2_codes, w2_scales, 1, 0)
        pack_half(w2_second, w2_codes, w2_scales, 1, 1)
        residual_on_vector(7, slice(BANK, WIDTH))
        residual_on_tensor(2)
        x2, x3 = new_pair(), new_pair()
        turn(x_sb, 4, x2, (scalar_copy, scalar_copy))
        products(0)
        residual_on_tensor(3)

        parts = {}

        def begin(first, gf):
            parts[first, gf] = (new_rows(), new_hidden())
            hidden_on_scalar(first, PAIR, gf, parts[first, gf][0], range(PACK))

        def lay(first, gf, copies):
            interleave(parts[first, gf][0], PAIR, parts[first, gf][1], copies)

        def quantise_part(first, gf):
            quantise_hidden(first, PAIR, gf, parts[first, gf][1])

        for i in range(ROW_TILES):
            sums(i)
            if i > 0:
                scaled(i - 1)
            if i == 0:
                pack_pair(x2, xb_codes, xb_scales, 0)
            if i in SUMMED_BY_SCALAR:
                averaged_on_scalar(i)
            else:
                averaged(i)
            if 2 <= i < 6:
                quantise_part(4 + (i - 2) // 2 * 2, i % 2)
            squared(i)
            if i in (2, 3):
                residual_on_tensor(i + 2)
            if i + 1 < ROW_TILES:
                products(i + 1)
            if i > 1:
                finished(i - 2)
            if i == 0:
                begin(4, 0)
            if i == 1:
                lay(4, 0, (vector_copy,))
                begin(4, 1)
                turn(x_sb, 6, x3, (scalar_copy, scalar_copy))
            if i == 2:
                lay(4, 1, (scalar_copy,))
                pack_pair(x3, xb_codes, xb_scales, 1)
                begin(6, 0)
            if i == 3:
                lay(6, 0, (scalar_copy,))
                begin(6, 1)
            if i == 4:
                lay(6, 1, (scalar_copy,))
            if i == 4:
                residual_on_tensor(6)
            if i == 5:
                residual_on_tensor(7, (0,))
            deviated(i)
        finished(6)
        scaled(7)
        finished(7, 2)
